import numpy as np
import ml_dtypes


def mxq(x, axis, fmt="e4m3"):
    dtype, down = {"e4m3": (ml_dtypes.float8_e4m3fn, 7), "e5m2": (ml_dtypes.float8_e5m2, 14)}[fmt]
    v = np.moveaxis(np.asarray(x, np.float32).astype(ml_dtypes.bfloat16).astype(np.float64), axis, -1)
    blocks = v.reshape(v.shape[:-1] + (-1, 32))
    amax = np.abs(blocks).max(-1, keepdims=True)
    byte = np.maximum(np.where(amax > 0, np.frexp(amax)[1] - 1 + 127, 0) - down, 1)
    scale = np.exp2(byte - 127.0)
    codes = (blocks / scale).astype(np.float32).astype(dtype).astype(np.float64)
    return np.moveaxis((codes * scale).reshape(v.shape), -1, axis)


WIDE = False


def mx_kscale(k):
    if not WIDE:
        return np.ones(k)
    levels = np.array([10, -10, 5, -5, 0])
    a = np.random.permutation(np.resize(levels, k // 512 * 4)).reshape(k // 512, 4)
    idx = np.arange(k)
    return np.exp2(a[idx // 512, idx % 128 // 32])


BF16 = ml_dtypes.bfloat16


def bf(x):
    return np.asarray(x, np.float32).astype(BF16)


def f64(x):
    return np.asarray(x).astype(np.float64)


G, B, NF, T, I, R, H = 1, 4096, 512, 512, 512, 1024, 256


def setup_inputs():
    kf, kt, kr = mx_kscale(NF), mx_kscale(T), mx_kscale(R)
    return {"v": bf(np.random.standard_normal((B, NF)) * kf),
            "s": bf(np.random.standard_normal((B, T)) * kt),
            "Ca": bf(np.random.standard_normal((G, NF, R)) / np.sqrt(NF) / kf[:, None] * kr),
            "Cb": bf(np.random.standard_normal((G, T, R)) / np.sqrt(T) / kt[:, None]),
            "Cc": bf(np.random.standard_normal((G, R, H)) * 0.7 / np.sqrt(R) / kr[:, None])}


def reference(v, s, Ca, Cb, Cc):
    t3 = mxq(f64(v), 1, "e4m3") @ mxq(f64(Ca), 1, "e4m3")
    t4 = mxq(f64(s), 1, "e4m3") @ mxq(f64(Cb), 1, "e4m3")
    return mxq(t3 * t4, 2, "e4m3") @ mxq(f64(Cc), 1, "e4m3")

@@ -1,0 +1,252 @@
+from contextlib import ExitStack
+
+import concourse.mybir as mybir
+from concourse.masks import make_identity
+
+F32 = mybir.dt.float32
+BF16 = mybir.dt.bfloat16
+U8 = mybir.dt.uint8
+U32 = mybir.dt.uint32
+FP8X4 = mybir.dt.float8_e4m3fn_x4
+
+P = 128
+B, K, R, H = 4096, 512, 1024, 256
+NSUB = B // P
+FLOPS = 2 * B * (2 * K * R + R * H)
+NPH = 16
+VSHARE = 352
+
+
+def tile_vnclcell_pa_t_kernel(tc, v, s, Ca, Cb, Cc, out):
+    nc = tc.nc
+    with ExitStack() as ctx:
+        keep = ctx.enter_context(tc.tile_pool(name="keep", bufs=1))
+        ring = ctx.enter_context(tc.tile_pool(name="ring", bufs=2))
+        psum = ctx.enter_context(tc.psum_pool(name="psum", bufs=1))
+        ctx.enter_context(tc.manual_schedule())
+
+        ident = keep.tile([P, P], F32, name="ident")
+        make_identity(nc, ident[:])
+
+        rows = {"v": v.rearrange("(p n) k -> p (n k)", n=NSUB), "s": s.rearrange("(p n) k -> p (n k)", n=NSUB)}
+        out_rows = out.rearrange("g (p n) h -> (g p) (n h)", n=NSUB)
+        wsrc = {"a": Ca, "b": Cb}
+
+        x_in = {}
+        for c in range(8):
+            for x in "vs":
+                x_in[x, c] = keep.tile([P, 4 * K], BF16, name="x_%s%d" % (x, c))
+        w_raw = {}
+        w_q = {}
+        w_s = {}
+        for w in "ab":
+            for g in range(2):
+                w_raw[w, g] = keep.tile([P, 4, 512], BF16, name="raw_%s%d" % (w, g))
+            w_q[w] = keep.tile([P, R], U32, name="wq_" + w, align_bytes=64)
+            w_s[w] = keep.tile([P, R], U8, name="ws_" + w, align_bytes=64)
+        c_raw = keep.tile([P, 8, H], BF16, name="raw_c")
+        c_q = keep.tile([P, 2 * H], U32, name="cq", align_bytes=64)
+        c_s = keep.tile([P, 2 * H], U8, name="cs", align_bytes=64)
+
+        def load_x(x, c, lo, hi):
+            nc.sync.dma_start(out=x_in[x, c][:, lo * K:hi * K], in_=rows[x][:, (4 * c + lo) * K:(4 * c + hi) * K])
+
+        def load_w(w, g):
+            for u in range(2):
+                nc.sync.dma_start(
+                    out=w_raw[w, g][:, 2 * u:2 * u + 2, :],
+                    in_=wsrc[w][0, 256 * u:256 * u + 256, 512 * g:512 * g + 512].rearrange("(q e) c -> q e c", e=2))
+
+        load_w("a", 0)
+        load_x("v", 0, 0, 2)
+        load_w("b", 0)
+        load_x("s", 0, 0, 2)
+        load_x("v", 0, 2, 4)
+        load_x("s", 0, 2, 4)
+        load_x("v", 1, 0, 2)
+        load_x("s", 1, 0, 2)
+        load_w("a", 1)
+        load_w("b", 1)
+        load_x("v", 1, 2, 4)
+        load_x("s", 1, 2, 4)
+        nc.sync.dma_start(out=c_raw[:], in_=Cc[0, :, :].rearrange("(a p) h -> p a h", p=P))
+        for c in range(2, 8):
+            load_x("v", c, 0, 4)
+            load_x("s", c, 0, 4)
+
+        def regroup(copy, dst, src):
+            copy(out=dst.rearrange("p (c i t) -> p c t i", i=4, t=4), in_=src.rearrange("p t (c i) -> p c t i", i=4))
+
+        grp = {}
+
+        def w_regroup(w, g):
+            grp[w, g] = ring.tile([P, 2048], BF16, name="grp", tag="grp", bufs=3, align_bytes=64)
+            regroup(nc.vector.tensor_copy, grp[w, g][:, 0:4 * VSHARE], w_raw[w, g][:, :, 0:VSHARE])
+            regroup(nc.scalar.copy, grp[w, g][:, 4 * VSHARE:2048], w_raw[w, g][:, :, VSHARE:512])
+
+        def w_quant(w, g):
+            nc.vector.quantize_mx(out=w_q[w][:, 512 * g:512 * g + 512].bitcast(FP8X4), scales=w_s[w][:, 512 * g:512 * g + 512],
+                                  in_=grp[w, g][:])
+
+        def c_regroup(copy):
+            grp["c"] = ring.tile([P, 2048], BF16, name="grp", tag="grp", bufs=3, align_bytes=64)
+            for g in range(2):
+                regroup(copy, grp["c"][:, 1024 * g:1024 * g + 1024], c_raw[:, 4 * g:4 * g + 4, :])
+
+        def c_quant():
+            nc.vector.quantize_mx(out=c_q[:].bitcast(FP8X4), scales=c_s[:], in_=grp["c"][:])
+
+        tb = {}
+        xg = {}
+        xq = {}
+        xs = {}
+
+        def T(t):
+            c, hp = divmod(t, 2)
+            for x in "vs":
+                tb[x, t] = psum.tile([P, 512], F32, name="tb", tag="m", bufs=2)
+                words = x_in[x, c][:].bitcast(F32)
+                for u in range(2):
+                    for i in range(2):
+                        nc.tensor.transpose(tb[x, t][:, 256 * u + 128 * i:256 * u + 128 * i + 128],
+                                            words[:, (2 * hp + i) * 256 + 128 * u:(2 * hp + i) * 256 + 128 * u + 128], ident[:])
+
+        def X(t, x, copy):
+            if x == "v":
+                xg[t] = ring.tile([P, 2048], BF16, name="xg", tag="xg", bufs=3, align_bytes=64)
+            o = 0 if x == "v" else 512
+            copy(out=xg[t][:].bitcast(F32)[:, o:o + 512].rearrange("p (c u) -> p c u", u=2),
+                 in_=tb[x, t][:].rearrange("p (u c) -> p c u", u=2))
+
+        def QX(t):
+            xq[t] = ring.tile([P, 512], U32, name="xq", tag="xq", bufs=6, align_bytes=64)
+            xs[t] = ring.tile([P, 512], U8, name="xs", tag="xs", bufs=6, align_bytes=64)
+            nc.vector.quantize_mx(out=xq[t][:].bitcast(FP8X4), scales=xs[t][:], in_=xg[t][:])
+
+        bank = {}
+        t3 = {}
+        pbf = {}
+        pq = {}
+        ps = {}
+
+        def U(f, nl):
+            c, g = divmod(f, 2)
+            t, i = 2 * c + nl // 2, nl % 2
+            for w, o, nb in (("a", 0, 3), ("b", 256, 3)):
+                bank[w, f, nl] = psum.tile([P, 512], F32, name="bk" + w, tag=w, bufs=nb)
+                for j in range(4):
+                    m = (4 * g + j) * P
+                    n = o + i * P
+                    nc.tensor.matmul_mx(out=bank[w, f, nl][:, j * P:(j + 1) * P],
+                                        lhsT=w_q[w][:, m:m + P].bitcast(FP8X4), lhsT_scale=w_s[w][:, m:m + P],
+                                        rhs=xq[t][:, n:n + P].bitcast(FP8X4), rhs_scale=xs[t][:, n:n + P],
+                                        start=True, stop=True)
+
+        def C(f, nl):
+            t3[f, nl] = ring.tile([P, 512], F32, name="t3", tag="t3", bufs=3)
+            nc.scalar.copy(out=t3[f, nl][:].rearrange("p (w j) -> p w j", j=4),
+                           in_=bank["a", f, nl][:].rearrange("p (j w) -> p w j", j=4))
+
+        def M(f, nl):
+            if nl == 0:
+                pbf[f] = ring.tile([P, 2048], BF16, name="pbf", tag="pbf", bufs=3, align_bytes=64)
+            nc.vector.tensor_tensor(out=pbf[f][:, 512 * nl:512 * nl + 512].rearrange("p (w j) -> p w j", j=4),
+                                    in0=bank["b", f, nl][:].rearrange("p (j w) -> p w j", j=4),
+                                    in1=t3[f, nl][:].rearrange("p (w j) -> p w j", j=4), op=mybir.AluOpType.mult)
+
+        def QP(f, lo=0, hi=4):
+            if lo == 0:
+                pq[f] = ring.tile([P, 512], U32, name="pq", tag="pq", bufs=6, align_bytes=64)
+                ps[f] = ring.tile([P, 512], U8, name="ps", tag="ps", bufs=6, align_bytes=64)
+            nc.vector.quantize_mx(out=pq[f][:, P * lo:P * hi].bitcast(FP8X4), scales=ps[f][:, P * lo:P * hi],
+                                  in_=pbf[f][:, 512 * lo:512 * hi])
+
+        ob = {}
+        osb = {}
+
+        def S3(c, lo, hi, tag="m", nb=2):
+            ob[c, lo] = psum.tile([P, 512], F32, name="ob", tag=tag, bufs=nb)
+            for nl in range(lo, hi):
+                for g in range(2):
+                    nc.tensor.matmul_mx(out=ob[c, lo][:, (nl - lo) * H:(nl - lo + 1) * H],
+                                        lhsT=pq[2 * c + g][:, nl * P:(nl + 1) * P].bitcast(FP8X4),
+                                        lhsT_scale=ps[2 * c + g][:, nl * P:(nl + 1) * P],
+                                        rhs=c_q[:, g * H:(g + 1) * H].bitcast(FP8X4), rhs_scale=c_s[:, g * H:(g + 1) * H],
+                                        start=(g == 0), stop=(g == 1))
+
+        def O(c, lo, hi, copy):
+            w = (hi - lo) * H
+            osb[c, lo] = ring.tile([P, 512], F32, name="osb", tag="osb", bufs=4)
+            copy(out=osb[c, lo][:, 0:w], in_=ob[c, lo][:, 0:w])
+            nc.sync.dma_start(out=out_rows[:, (4 * c + lo) * H:(4 * c + hi) * H], in_=osb[c, lo][:, 0:w])
+
+        vcopy = nc.vector.tensor_copy
+        scopy = nc.scalar.copy
+
+        w_regroup("a", 0)
+        T(0)
+        X(0, "v", scopy)
+        w_regroup("b", 0)
+        w_quant("a", 0)
+        X(0, "s", scopy)
+        T(1)
+        w_quant("b", 0)
+        QX(0)
+        X(1, "v", scopy)
+        X(1, "s", scopy)
+
+        def job(q):
+            S3(q // 2, 2 * (q % 2), 2 * (q % 2) + 2)
+
+        def job_out(q):
+            O(q // 2, 2 * (q % 2), 2 * (q % 2) + 2, scopy)
+
+        for f in range(NPH):
+            t = f + 2
+            more = t < NPH
+            q = f - 3
+            if more:
+                T(t)
+                X(t, "v", scopy)
+            U(f, 0)
+            C(f, 0)
+            if f == 0:
+                QX(1)
+            U(f, 1)
+            C(f, 1)
+            M(f, 0)
+            if f == 0:
+                w_regroup("a", 1)
+            if more:
+                X(t, "s", scopy)
+            if q >= 0:
+                job(q)
+            M(f, 1)
+            if f >= 1:
+                QP(f - 1)
+            if f == 0:
+                w_regroup("b", 1)
+                w_quant("a", 1)
+            U(f, 2)
+            C(f, 2)
+            if q >= 0:
+                job_out(q)
+            M(f, 2)
+            if f == 0:
+                w_quant("b", 1)
+            if more:
+                QX(t)
+            if f == 1:
+                c_regroup(vcopy)
+            U(f, 3)
+            C(f, 3)
+            M(f, 3)
+            if f == 2:
+                c_quant()
+        job(13)
+        job_out(13)
+        QP(NPH - 1)
+        job(14)
+        job(15)
+        job_out(14)
+        O(7, 2, 4, vcopy)

@@ -15,6 +15,10 @@ NSUB = B // P
 FLOPS = 2 * B * (2 * K * R + R * H)
 NPH = 16
 VSHARE = 352
+SPEC = {"banks":[3,3,2],"head":{"P":[["T",0],["T",1]],"S":[["RW","a",0],["Xv",0],["RW","b",0],["Xs",0],["Xv",1],["Xs",1]],"V":[["RW","a",0],["RW","b",0],["QW","a",0],["QW","b",0],["QX",0]]},"phase":{"P":[["T",{"d":2}],["A",{"d":0},0],["B",{"d":0},0],["A",{"d":0},1],["B",{"d":0},1],["S3",{"d":-4}],["A",{"d":0},2],["B",{"d":0},2],["A",{"d":0},3],["B",{"d":0},3]],"S":[["Xv",{"d":2}],["Xs",{"d":2}],["C",{"d":0},0],["C",{"d":0},1],["O",{"d":-4}],["C",{"d":0},2],["C",{"d":0},3]],"V":[["M",{"d":0},0],["M",{"d":0},1],["QP",{"d":-2}],["M",{"d":0},2],["QX",{"d":2}],["M",{"d":0},3]]},"phase_special":{"0":{"P":[["A",{"d":0},0],["B",{"d":0},0],["A",{"d":0},1],["B",{"d":0},1],["T",{"d":2}],["A",{"d":0},2],["B",{"d":0},2],["A",{"d":0},3],["B",{"d":0},3]],"S":[["C",{"d":0},0],["C",{"d":0},1],["RW","a",1],["Xv",{"d":2}],["Xs",{"d":2}],["RW","b",1],["C",{"d":0},2],["C",{"d":0},3]],"V":[["QX",1],["M",{"d":0},0],["RW","a",1],["M",{"d":0},1],["RW","b",1],["QW","a",1],["M",{"d":0},2],["QW","b",1],["QX",{"d":2}],["M",{"d":0},3]]},"1":{"V":[["M",{"d":0},0],["M",{"d":0},1],["RC"],["M",{"d":0},2],["QX",{"d":2}],["M",{"d":0},3]]},"2":{"V":[["M",{"d":0},0],["M",{"d":0},1],["QP",{"d":-2}],["M",{"d":0},2],["QX",{"d":2}],["M",{"d":0},3]]},"3":{"V":[["M",{"d":0},0],["M",{"d":0},1],["QP",{"d":-2}],["M",{"d":0},2],["QX",{"d":2}],["QC"],["M",{"d":0},3]]},"14":{"P":[["A",14,0],["B",14,0],["S3",10],["A",14,1],["B",14,1],["A",14,2],["B",14,2],["S3",11],["A",14,3],["B",14,3]],"S":[["C",14,0],["O",10],["C",14,1],["C",14,2],["O",11],["C",14,3]],"V":[["M",14,0],["QP",12],["M",14,1],["QP",13],["M",14,2],["M",14,3]]},"15":{"P":[["A",15,0],["B",15,0],["S3",12],["A",15,1],["B",15,1],["A",15,2],["B",15,2],["S3",13],["A",15,3],["B",15,3]],"S":[["C",15,0],["O",12],["C",15,1],["C",15,2],["O",13],["C",15,3]],"V":[["M",15,0],["QP",14],["M",15,1],["M",15,2],["QPa",15],["M",15,3],["QPc",15],["QPd",15]]}},"tail":{"P":[["S3",14],["S3h",2],["S3h",3]],"S":[["O",14],["Oh",2]],"V":[["Ohv",3]]},"vshare":[352,352,1],"pbf":4,"pq":6}
+NA = 3
+NB = 3
+NM = 2
 
 
 def tile_vnclcell_pa_t_kernel(tc, v, s, Ca, Cb, Cc, out):
@@ -81,8 +85,9 @@ def tile_vnclcell_pa_t_kernel(tc, v, s, Ca, Cb, Cc, out):
 
         def w_regroup(w, g):
             grp[w, g] = ring.tile([P, 2048], BF16, name="grp", tag="grp", bufs=3, align_bytes=64)
-            regroup(nc.vector.tensor_copy, grp[w, g][:, 0:4 * VSHARE], w_raw[w, g][:, :, 0:VSHARE])
-            regroup(nc.scalar.copy, grp[w, g][:, 4 * VSHARE:2048], w_raw[w, g][:, :, VSHARE:512])
+            vs = SPEC["vshare"][g]
+            regroup(nc.vector.tensor_copy, grp[w, g][:, 0:4 * vs], w_raw[w, g][:, :, 0:vs])
+            regroup(nc.scalar.copy, grp[w, g][:, 4 * vs:2048], w_raw[w, g][:, :, vs:512])
 
         def w_quant(w, g):
             nc.vector.quantize_mx(out=w_q[w][:, 512 * g:512 * g + 512].bitcast(FP8X4), scales=w_s[w][:, 512 * g:512 * g + 512],
@@ -90,8 +95,8 @@ def tile_vnclcell_pa_t_kernel(tc, v, s, Ca, Cb, Cc, out):
 
         def c_regroup(copy):
             grp["c"] = ring.tile([P, 2048], BF16, name="grp", tag="grp", bufs=3, align_bytes=64)
-            for g in range(2):
-                regroup(copy, grp["c"][:, 1024 * g:1024 * g + 1024], c_raw[:, 4 * g:4 * g + 4, :])
+            regroup(nc.vector.tensor_copy, grp["c"][:, 0:1024], c_raw[:, 0:4, :])
+            regroup(nc.vector.tensor_copy if SPEC["vshare"][2] else nc.scalar.copy, grp["c"][:, 1024:2048], c_raw[:, 4:8, :])
 
         def c_quant():
             nc.vector.quantize_mx(out=c_q[:].bitcast(FP8X4), scales=c_s[:], in_=grp["c"][:])
@@ -104,7 +109,7 @@ def tile_vnclcell_pa_t_kernel(tc, v, s, Ca, Cb, Cc, out):
         def T(t):
             c, hp = divmod(t, 2)
             for x in "vs":
-                tb[x, t] = psum.tile([P, 512], F32, name="tb", tag="m", bufs=2)
+                tb[x, t] = psum.tile([P, 512], F32, name="tb", tag="m", bufs=NM)
                 words = x_in[x, c][:].bitcast(F32)
                 for u in range(2):
                     for i in range(2):
@@ -129,10 +134,10 @@ def tile_vnclcell_pa_t_kernel(tc, v, s, Ca, Cb, Cc, out):
         pq = {}
         ps = {}
 
-        def U(f, nl):
+        def U(f, nl, which):
             c, g = divmod(f, 2)
             t, i = 2 * c + nl // 2, nl % 2
-            for w, o, nb in (("a", 0, 3), ("b", 256, 3)):
+            for w, o, nb in ((("a", 0, NA),) if which == "a" else (("b", 256, NB),)):
                 bank[w, f, nl] = psum.tile([P, 512], F32, name="bk" + w, tag=w, bufs=nb)
                 for j in range(4):
                     m = (4 * g + j) * P
@@ -149,22 +154,22 @@ def tile_vnclcell_pa_t_kernel(tc, v, s, Ca, Cb, Cc, out):
 
         def M(f, nl):
             if nl == 0:
-                pbf[f] = ring.tile([P, 2048], BF16, name="pbf", tag="pbf", bufs=3, align_bytes=64)
+                pbf[f] = ring.tile([P, 2048], BF16, name="pbf", tag="pbf", bufs=SPEC.get("pbf", 3), align_bytes=64)
             nc.vector.tensor_tensor(out=pbf[f][:, 512 * nl:512 * nl + 512].rearrange("p (w j) -> p w j", j=4),
                                     in0=bank["b", f, nl][:].rearrange("p (j w) -> p w j", j=4),
                                     in1=t3[f, nl][:].rearrange("p (w j) -> p w j", j=4), op=mybir.AluOpType.mult)
 
         def QP(f, lo=0, hi=4):
             if lo == 0:
-                pq[f] = ring.tile([P, 512], U32, name="pq", tag="pq", bufs=6, align_bytes=64)
-                ps[f] = ring.tile([P, 512], U8, name="ps", tag="ps", bufs=6, align_bytes=64)
+                pq[f] = ring.tile([P, 512], U32, name="pq", tag="pq", bufs=SPEC.get("pq", 6), align_bytes=64)
+                ps[f] = ring.tile([P, 512], U8, name="ps", tag="ps", bufs=SPEC.get("pq", 6), align_bytes=64)
             nc.vector.quantize_mx(out=pq[f][:, P * lo:P * hi].bitcast(FP8X4), scales=ps[f][:, P * lo:P * hi],
                                   in_=pbf[f][:, 512 * lo:512 * hi])
 
         ob = {}
         osb = {}
 
-        def S3(c, lo, hi, tag="m", nb=2):
+        def S3(c, lo, hi, tag="m", nb=NM):
             ob[c, lo] = psum.tile([P, 512], F32, name="ob", tag=tag, bufs=nb)
             for nl in range(lo, hi):
                 for g in range(2):
@@ -183,70 +188,141 @@ def tile_vnclcell_pa_t_kernel(tc, v, s, Ca, Cb, Cc, out):
         vcopy = nc.vector.tensor_copy
         scopy = nc.scalar.copy
 
-        w_regroup("a", 0)
-        T(0)
-        X(0, "v", scopy)
-        w_regroup("b", 0)
-        w_quant("a", 0)
-        X(0, "s", scopy)
-        T(1)
-        w_quant("b", 0)
-        QX(0)
-        X(1, "v", scopy)
-        X(1, "s", scopy)
+        ops = {}
+        def add(key, eng, fn, pre):
+            ops[key] = (eng, fn, pre)
+        for w in "ab":
+            for g in range(2):
+                add(("RW", w, g), "VS", (lambda w=w, g=g: w_regroup(w, g)), [])
+                add(("QW", w, g), "V", (lambda w=w, g=g: w_quant(w, g)), [("RW", w, g)])
+        add(("RC",), "V", (lambda: c_regroup(vcopy)), [])
+        add(("QC",), "V", c_quant, [("RC",)])
+        for t in range(16):
+            add(("T", t), "P", (lambda t=t: T(t)), [])
+            add(("Xv", t), "S", (lambda t=t: X(t, "v", scopy)), [("T", t)])
+            add(("Xs", t), "S", (lambda t=t: X(t, "s", scopy)), [("T", t), ("Xv", t)])
+            add(("QX", t), "V", (lambda t=t: QX(t)), [("Xs", t)])
+        for f in range(16):
+            c, g = divmod(f, 2)
+            for nl in range(4):
+                t = 2 * c + nl // 2
+                add(("A", f, nl), "P", (lambda f=f, nl=nl: U(f, nl, "a")), [("QX", t), ("QW", "a", g)])
+                add(("B", f, nl), "P", (lambda f=f, nl=nl: U(f, nl, "b")), [("QX", t), ("QW", "b", g)])
+                add(("C", f, nl), "S", (lambda f=f, nl=nl: C(f, nl)), [("A", f, nl)])
+                add(("M", f, nl), "V", (lambda f=f, nl=nl: M(f, nl)), [("C", f, nl), ("B", f, nl)] + ([("M", f, nl - 1)] if nl else []))
+            add(("QP", f), "V", (lambda f=f: QP(f)), [("M", f, 3)])
+            add(("QPa", f), "V", (lambda f=f: QP(f, 0, 2)), [("M", f, 1)])
+            add(("QPb", f), "V", (lambda f=f: QP(f, 2, 4)), [("M", f, 3), ("QPa", f)])
+            add(("QPc", f), "V", (lambda f=f: QP(f, 2, 3)), [("M", f, 2), ("QPa", f)])
+            add(("QPd", f), "V", (lambda f=f: QP(f, 3, 4)), [("M", f, 3), ("QPc", f)])
+        for q in range(16):
+            c = q // 2
+            add(("S3", q), "P", (lambda q=q: S3(q // 2, 2 * (q % 2), 2 * (q % 2) + 2)), [("QPx", 2 * c, q % 2), ("QPx", 2 * c + 1, q % 2), ("QC",)])
+            add(("O", q), "S", (lambda q=q: O(q // 2, 2 * (q % 2), 2 * (q % 2) + 2, scopy)), [("S3", q)])
+            add(("Ov", q), "V", (lambda q=q: O(q // 2, 2 * (q % 2), 2 * (q % 2) + 2, vcopy)), [("S3", q)])
+        for nl in (2, 3):
+            add(("S3h", nl), "P", (lambda nl=nl: S3(7, nl, nl + 1)), [("QPx", 14, 1), ("QPy", 15, nl), ("QC",)])
+            add(("Oh", nl), "S", (lambda nl=nl: O(7, nl, nl + 1, scopy)), [("S3h", nl)])
+            add(("Ohv", nl), "V", (lambda nl=nl: O(7, nl, nl + 1, vcopy)), [("S3h", nl)])
 
-        def job(q):
-            S3(q // 2, 2 * (q % 2), 2 * (q % 2) + 2)
+        def expand(seq, f):
+            res = []
+            for item in seq:
+                nm, args = item[0], item[1:]
+                key = tuple([nm] + [(f + a["d"] if isinstance(a, dict) else a) for a in args])
+                res.append(key)
+            return res
 
-        def job_out(q):
-            O(q // 2, 2 * (q % 2), 2 * (q % 2) + 2, scopy)
+        queues = {"P": [], "S": [], "V": []}
+        for e in "PSV":
+            for key in SPEC["head"][e]:
+                queues[e].append(tuple(key))
+        for f in range(16):
+            for e in "PSV":
+                spec = SPEC["phase_special"].get(str(f), {}).get(e) or SPEC["phase"][e]
+                for key in expand(spec, f):
+                    if key[0] in ("T", "Xv", "Xs", "QX") and not (0 <= key[1] < 16): continue
+                    if key[0] in ("S3", "O", "Ov") and not (0 <= key[1] < 16): continue
+                    if key[0] in ("QP",) and not (0 <= key[1] < 16): continue
+                    queues[e].append(key)
+        for e in "PSV":
+            for key in SPEC["tail"][e]:
+                queues[e].append(tuple(key))
+        done = set()
 
-        for f in range(NPH):
-            t = f + 2
-            more = t < NPH
-            q = f - 3
-            if more:
-                T(t)
-                X(t, "v", scopy)
-            U(f, 0)
-            C(f, 0)
-            if f == 0:
-                QX(1)
-            U(f, 1)
-            C(f, 1)
-            M(f, 0)
-            if f == 0:
-                w_regroup("a", 1)
-            if more:
-                X(t, "s", scopy)
-            if q >= 0:
-                job(q)
-            M(f, 1)
-            if f >= 1:
-                QP(f - 1)
-            if f == 0:
-                w_regroup("b", 1)
-                w_quant("a", 1)
-            U(f, 2)
-            C(f, 2)
-            if q >= 0:
-                job_out(q)
-            M(f, 2)
-            if f == 0:
-                w_quant("b", 1)
-            if more:
-                QX(t)
-            if f == 1:
-                c_regroup(vcopy)
-            U(f, 3)
-            C(f, 3)
-            M(f, 3)
-            if f == 2:
-                c_quant()
-        job(13)
-        job_out(13)
-        QP(NPH - 1)
-        job(14)
-        job(15)
-        job_out(14)
-        O(7, 2, 4, vcopy)
+        def sat(p):
+            if p[0] == "QPx":
+                return ("QP", p[1]) in done or (("QPa", p[1]) in done if p[2] == 0 else (("QPb", p[1]) in done or ("QPd", p[1]) in done))
+            if p[0] == "QPy":
+                return ("QP", p[1]) in done or ("QPb", p[1]) in done or (("QPc", p[1]) in done if p[2] == 2 else ("QPd", p[1]) in done)
+            if p[0] == "Oany":
+                return ("O", p[1]) in done or ("Ov", p[1]) in done
+            if p[0] == "Ohany":
+                return ("Oh", p[1]) in done or ("Ohv", p[1]) in done
+            return p in done
+
+        m_readers = []
+        grp_users = []
+
+        def reuse(key):
+            k = key[0]
+            res = []
+            if k in ("A", "B", "C"):
+                n = 4 * key[1] + key[2]
+                back = {"A": NA, "B": NB, "C": 3}[k]
+                if n - back >= 0:
+                    res.append(({"A": "C", "B": "M", "C": "M"}[k], (n - back) // 4, (n - back) % 4))
+            if k in ("T", "S3", "S3h"):
+                need = 2 if k == "T" else 1
+                for i in range(need):
+                    j = len(m_readers) + i - NM
+                    if j >= 0:
+                        res.append(m_readers[j] if j < len(m_readers) else ("never",))
+            if k == "Xv" and key[1] >= 3:
+                res.append(("QX", key[1] - 3))
+            if k == "QX" and key[1] >= 6:
+                t = key[1] - 6
+                res.append(("B", 2 * (t // 2) + 1, 2 * (t % 2) + 1))
+            if k == "M" and key[2] == 0 and key[1] >= SPEC.get("pbf", 3):
+                res.append(("QPx", key[1] - SPEC.get("pbf", 3), 1))
+            if k in ("QP", "QPa") and key[1] >= SPEC.get("pq", 6):
+                res.append(("S3", 2 * ((key[1] - SPEC.get("pq", 6)) // 2) + 1))
+            if k in ("RW", "RC") and len(grp_users) >= 3:
+                res.append(grp_users[len(grp_users) - 3])
+            return res
+
+        def emitted(key):
+            k = key[0]
+            if k == "T":
+                m_readers.append(("Xv", key[1]))
+                m_readers.append(("Xs", key[1]))
+            if k == "S3":
+                m_readers.append(("Oany", key[1]))
+            if k == "S3h":
+                m_readers.append(("Ohany", key[1]))
+            if k == "RW":
+                grp_users.append(("QW", key[1], key[2]))
+            if k == "RC":
+                grp_users.append(("QC",))
+            done.add(key)
+
+        pos = {"P": 0, "S": 0, "V": 0}
+        while any(pos[e] < len(queues[e]) for e in "PSV"):
+            prog = False
+            for e in "PSV":
+                if pos[e] >= len(queues[e]):
+                    continue
+                key = queues[e][pos[e]]
+                eng, fn, prq = ops[key]
+                if not all(sat(p) for p in list(prq) + reuse(key)):
+                    continue
+                if key[0] == "RW" or (key[0] == "RC" and not SPEC["vshare"][2]):
+                    other = "S" if e == "V" else "V"
+                    if not (pos[other] < len(queues[other]) and queues[other][pos[other]] == key):
+                        continue
+                    pos[other] += 1
+                fn()
+                emitted(key)
+                pos[e] += 1
+                prog = True
+            assert prog, "the three orders cannot be merged"

@@ -15,7 +15,7 @@ NSUB = B // P
 FLOPS = 2 * B * (2 * K * R + R * H)
 NPH = 16
 VSHARE = 352
-SPEC = {"banks":[3,3,2],"head":{"P":[["T",0],["T",1]],"S":[["RW","a",0],["Xv",0],["RW","b",0],["Xs",0],["Xv",1],["Xs",1]],"V":[["RW","a",0],["RW","b",0],["QW","a",0],["QW","b",0],["QX",0]]},"phase":{"P":[["T",{"d":2}],["A",{"d":0},0],["B",{"d":0},0],["A",{"d":0},1],["B",{"d":0},1],["S3",{"d":-4}],["A",{"d":0},2],["B",{"d":0},2],["A",{"d":0},3],["B",{"d":0},3]],"S":[["Xv",{"d":2}],["Xs",{"d":2}],["C",{"d":0},0],["C",{"d":0},1],["O",{"d":-4}],["C",{"d":0},2],["C",{"d":0},3]],"V":[["M",{"d":0},0],["M",{"d":0},1],["QP",{"d":-2}],["M",{"d":0},2],["QX",{"d":2}],["M",{"d":0},3]]},"phase_special":{"0":{"P":[["A",{"d":0},0],["B",{"d":0},0],["A",{"d":0},1],["B",{"d":0},1],["T",{"d":2}],["A",{"d":0},2],["B",{"d":0},2],["A",{"d":0},3],["B",{"d":0},3]],"S":[["C",{"d":0},0],["C",{"d":0},1],["RW","a",1],["Xv",{"d":2}],["Xs",{"d":2}],["RW","b",1],["C",{"d":0},2],["C",{"d":0},3]],"V":[["QX",1],["M",{"d":0},0],["RW","a",1],["M",{"d":0},1],["RW","b",1],["QW","a",1],["M",{"d":0},2],["QW","b",1],["QX",{"d":2}],["M",{"d":0},3]]},"1":{"V":[["M",{"d":0},0],["M",{"d":0},1],["RC"],["M",{"d":0},2],["QX",{"d":2}],["M",{"d":0},3]]},"2":{"V":[["M",{"d":0},0],["M",{"d":0},1],["QP",{"d":-2}],["M",{"d":0},2],["QX",{"d":2}],["M",{"d":0},3]]},"3":{"V":[["M",{"d":0},0],["M",{"d":0},1],["QP",{"d":-2}],["M",{"d":0},2],["QX",{"d":2}],["QC"],["M",{"d":0},3]]},"14":{"P":[["A",14,0],["B",14,0],["S3",10],["A",14,1],["B",14,1],["A",14,2],["B",14,2],["S3",11],["A",14,3],["B",14,3]],"S":[["C",14,0],["O",10],["C",14,1],["C",14,2],["O",11],["C",14,3]],"V":[["M",14,0],["QP",12],["M",14,1],["QP",13],["M",14,2],["M",14,3]]},"15":{"P":[["A",15,0],["B",15,0],["S3",12],["A",15,1],["B",15,1],["A",15,2],["B",15,2],["S3",13],["A",15,3],["B",15,3]],"S":[["C",15,0],["O",12],["C",15,1],["C",15,2],["O",13],["C",15,3]],"V":[["M",15,0],["QP",14],["M",15,1],["M",15,2],["QPa",15],["M",15,3],["QPc",15],["QPd",15]]}},"tail":{"P":[["S3",14],["S3h",2],["S3h",3]],"S":[["O",14],["Oh",2]],"V":[["Ohv",3]]},"vshare":[352,352,1],"pbf":4,"pq":6}
+SPEC = {"banks":[3,3,2],"head":{"P":[["T",0],["T",1],["A",0,0],["A",0,1]],"S":[["RW","a",0],["Xv",0],["RW","b",0],["Xs",0],["Xv",1],["Xs",1],["C",0,0],["C",0,1]],"V":[["RW","a",0],["RW","b",0],["QW","a",0],["QX",0],["QW","b",0]]},"phase":{"P":[["T",{"d":2}],["A",{"d":0},2],["B",{"d":0},0],["A",{"d":0},3],["B",{"d":0},1],["S3",{"d":-4}],["A",{"d":1},0],["B",{"d":0},2],["A",{"d":1},1],["B",{"d":0},3]],"S":[["Xv",{"d":2}],["Xs",{"d":2}],["C",{"d":0},2],["C",{"d":0},3],["O",{"d":-4}],["C",{"d":1},0],["C",{"d":1},1]],"V":[["M",{"d":0},0],["QX",{"d":2}],["M",{"d":0},1],["QP",{"d":-2}],["M",{"d":0},2],["M",{"d":0},3]]},"phase_special":{"0":{"P":[["B",0,0],["B",0,1],["A",0,2],["A",0,3],["T",2],["B",0,2],["B",0,3],["A",1,0],["A",1,1]],"S":[["RW","a",1],["C",0,2],["C",0,3],["Xv",2],["Xs",2],["RW","b",1],["C",1,0],["C",1,1]],"V":[["QX",1],["M",0,0],["RW","a",1],["M",0,1],["QW","a",1],["M",0,2],["RW","b",1],["QX",2],["QW","b",1],["M",0,3]]},"1":{"V":[["M",{"d":0},0],["QX",{"d":2}],["M",{"d":0},1],["RC"],["M",{"d":0},2],["M",{"d":0},3]]},"3":{"V":[["M",{"d":0},0],["QX",{"d":2}],["M",{"d":0},1],["QP",{"d":-2}],["M",{"d":0},2],["QC"],["M",{"d":0},3]]},"14":{"P":[["A",14,2],["B",14,0],["A",14,3],["B",14,1],["S3",10],["A",15,0],["B",14,2],["A",15,1],["B",14,3],["S3",11],["A",15,2],["B",15,0],["A",15,3],["B",15,1],["S3",12],["B",15,2],["B",15,3],["S3",13],["S3",14],["S3h",2],["S3h",3]],"S":[["C",14,2],["C",14,3],["O",10],["C",15,0],["C",15,1],["O",11],["C",15,2],["C",15,3],["O",12],["O",13],["O",14],["Oh",2]],"V":[["M",14,0],["QP",12],["M",14,1],["QP",13],["M",14,2],["M",14,3],["M",15,0],["M",15,1],["QP",14],["QPa",15],["M",15,2],["M",15,3],["QPc",15],["QPd",15],["Ohv",3]]},"15":{"P":[["NOP"]],"S":[["NOP"]],"V":[["NOP"]]}},"tail":{"P":[],"S":[],"V":[]},"vshare":[352,352,1],"pbf":4,"pq":6,"dma":[["w","a",0],["x","v",0,0,2],["w","b",0],["x","s",0,0,2],["x","v",0,2,4],["x","s",0,2,4],["x","v",1,0,2],["x","s",1,0,2],["w","a",1],["w","b",1],["x","v",1,2,4],["x","s",1,2,4],["c"]],"t3":6}
 NA = 3
 NB = 3
 NM = 2
@@ -61,19 +61,13 @@ def tile_vnclcell_pa_t_kernel(tc, v, s, Ca, Cb, Cc, out):
                     out=w_raw[w, g][:, 2 * u:2 * u + 2, :],
                     in_=wsrc[w][0, 256 * u:256 * u + 256, 512 * g:512 * g + 512].rearrange("(q e) c -> q e c", e=2))
 
-        load_w("a", 0)
-        load_x("v", 0, 0, 2)
-        load_w("b", 0)
-        load_x("s", 0, 0, 2)
-        load_x("v", 0, 2, 4)
-        load_x("s", 0, 2, 4)
-        load_x("v", 1, 0, 2)
-        load_x("s", 1, 0, 2)
-        load_w("a", 1)
-        load_w("b", 1)
-        load_x("v", 1, 2, 4)
-        load_x("s", 1, 2, 4)
-        nc.sync.dma_start(out=c_raw[:], in_=Cc[0, :, :].rearrange("(a p) h -> p a h", p=P))
+        for item in SPEC["dma"]:
+            if item[0] == "w":
+                load_w(item[1], item[2])
+            elif item[0] == "x":
+                load_x(item[1], item[2], item[3], item[4])
+            else:
+                nc.sync.dma_start(out=c_raw[:], in_=Cc[0, :, :].rearrange("(a p) h -> p a h", p=P))
         for c in range(2, 8):
             load_x("v", c, 0, 4)
             load_x("s", c, 0, 4)
@@ -148,7 +142,7 @@ def tile_vnclcell_pa_t_kernel(tc, v, s, Ca, Cb, Cc, out):
                                         start=True, stop=True)
 
         def C(f, nl):
-            t3[f, nl] = ring.tile([P, 512], F32, name="t3", tag="t3", bufs=3)
+            t3[f, nl] = ring.tile([P, 512], F32, name="t3", tag="t3", bufs=SPEC.get("t3", 3))
             nc.scalar.copy(out=t3[f, nl][:].rearrange("p (w j) -> p w j", j=4),
                            in_=bank["a", f, nl][:].rearrange("p (j w) -> p w j", j=4))
 
@@ -241,9 +235,10 @@ def tile_vnclcell_pa_t_kernel(tc, v, s, Ca, Cb, Cc, out):
             for e in "PSV":
                 spec = SPEC["phase_special"].get(str(f), {}).get(e) or SPEC["phase"][e]
                 for key in expand(spec, f):
+                    if key[0] == "NOP": continue
                     if key[0] in ("T", "Xv", "Xs", "QX") and not (0 <= key[1] < 16): continue
                     if key[0] in ("S3", "O", "Ov") and not (0 <= key[1] < 16): continue
-                    if key[0] in ("QP",) and not (0 <= key[1] < 16): continue
+                    if key[0] in ("QP", "A", "B", "C", "M") and not (0 <= key[1] < 16): continue
                     queues[e].append(key)
         for e in "PSV":
             for key in SPEC["tail"][e]:
@@ -269,7 +264,7 @@ def tile_vnclcell_pa_t_kernel(tc, v, s, Ca, Cb, Cc, out):
             res = []
             if k in ("A", "B", "C"):
                 n = 4 * key[1] + key[2]
-                back = {"A": NA, "B": NB, "C": 3}[k]
+                back = {"A": NA, "B": NB, "C": SPEC.get("t3", 3)}[k]
                 if n - back >= 0:
                     res.append(({"A": "C", "B": "M", "C": "M"}[k], (n - back) // 4, (n - back) % 4))
             if k in ("T", "S3", "S3h"):

@@ -15,7 +15,7 @@ NSUB = B // P
 FLOPS = 2 * B * (2 * K * R + R * H)
 NPH = 16
 VSHARE = 352
-SPEC = {"banks":[3,3,2],"head":{"P":[["T",0],["T",1],["A",0,0],["A",0,1]],"S":[["RW","a",0],["Xv",0],["RW","b",0],["Xs",0],["Xv",1],["Xs",1],["C",0,0],["C",0,1]],"V":[["RW","a",0],["RW","b",0],["QW","a",0],["QX",0],["QW","b",0]]},"phase":{"P":[["T",{"d":2}],["A",{"d":0},2],["B",{"d":0},0],["A",{"d":0},3],["B",{"d":0},1],["S3",{"d":-4}],["A",{"d":1},0],["B",{"d":0},2],["A",{"d":1},1],["B",{"d":0},3]],"S":[["Xv",{"d":2}],["Xs",{"d":2}],["C",{"d":0},2],["C",{"d":0},3],["O",{"d":-4}],["C",{"d":1},0],["C",{"d":1},1]],"V":[["M",{"d":0},0],["QX",{"d":2}],["M",{"d":0},1],["QP",{"d":-2}],["M",{"d":0},2],["M",{"d":0},3]]},"phase_special":{"0":{"P":[["B",0,0],["B",0,1],["A",0,2],["A",0,3],["T",2],["B",0,2],["B",0,3],["A",1,0],["A",1,1]],"S":[["RW","a",1],["C",0,2],["C",0,3],["Xv",2],["Xs",2],["RW","b",1],["C",1,0],["C",1,1]],"V":[["QX",1],["M",0,0],["RW","a",1],["M",0,1],["QW","a",1],["M",0,2],["RW","b",1],["QX",2],["QW","b",1],["M",0,3]]},"1":{"V":[["M",{"d":0},0],["QX",{"d":2}],["M",{"d":0},1],["RC"],["M",{"d":0},2],["M",{"d":0},3]]},"3":{"V":[["M",{"d":0},0],["QX",{"d":2}],["M",{"d":0},1],["QP",{"d":-2}],["M",{"d":0},2],["QC"],["M",{"d":0},3]]},"14":{"P":[["A",14,2],["B",14,0],["A",14,3],["B",14,1],["S3",10],["A",15,0],["B",14,2],["A",15,1],["B",14,3],["S3",11],["A",15,2],["B",15,0],["A",15,3],["B",15,1],["S3",12],["B",15,2],["B",15,3],["S3",13],["S3",14],["S3h",2],["S3h",3]],"S":[["C",14,2],["C",14,3],["O",10],["C",15,0],["C",15,1],["O",11],["C",15,2],["C",15,3],["O",12],["O",13],["O",14],["Oh",2]],"V":[["M",14,0],["QP",12],["M",14,1],["QP",13],["M",14,2],["M",14,3],["M",15,0],["M",15,1],["QP",14],["QPa",15],["M",15,2],["M",15,3],["QPc",15],["QPd",15],["Ohv",3]]},"15":{"P":[["NOP"]],"S":[["NOP"]],"V":[["NOP"]]}},"tail":{"P":[],"S":[],"V":[]},"vshare":[352,352,1],"pbf":4,"pq":6,"dma":[["w","a",0],["x","v",0,0,2],["w","b",0],["x","s",0,0,2],["x","v",0,2,4],["x","s",0,2,4],["x","v",1,0,2],["x","s",1,0,2],["w","a",1],["w","b",1],["x","v",1,2,4],["x","s",1,2,4],["c"]],"t3":6}
+SPEC = {"banks":[3,3,2],"head":{"P":[["T",0],["T",1],["A",0,0],["A",0,1]],"S":[["RW","a",0],["Xv",0],["RW","b",0],["Xs",0],["Xv",1],["Xs",1],["C",0,0],["C",0,1]],"V":[["RW","a",0],["RW","b",0],["QW","a",0],["QX",0],["QW","b",0]]},"phase":{"P":[["T",{"d":2}],["A",{"d":0},2],["B",{"d":0},0],["A",{"d":0},3],["B",{"d":0},1],["S3",{"d":-4}],["A",{"d":1},0],["B",{"d":0},2],["A",{"d":1},1],["B",{"d":0},3]],"S":[["Xv",{"d":2}],["Xs",{"d":2}],["C",{"d":0},2],["C",{"d":0},3],["O",{"d":-4}],["C",{"d":1},0],["C",{"d":1},1]],"V":[["M",{"d":0},0],["QX",{"d":2}],["M",{"d":0},1],["M",{"d":0},2],["QP",{"d":-2}],["M",{"d":0},3]]},"phase_special":{"0":{"P":[["B",0,0],["B",0,1],["A",0,2],["A",0,3],["T",2],["B",0,2],["B",0,3],["A",1,0],["A",1,1]],"S":[["RW","a",1],["C",0,2],["C",0,3],["Xv",2],["Xs",2],["RW","b",1],["C",1,0],["C",1,1]],"V":[["QX",1],["RW","a",1],["M",0,0],["M",0,1],["QW","a",1],["RW","b",1],["M",0,2],["QX",2],["QW","b",1],["M",0,3]]},"1":{"V":[["M",{"d":0},0],["QX",{"d":2}],["M",{"d":0},1],["RC"],["M",{"d":0},2],["M",{"d":0},3]]},"3":{"V":[["M",{"d":0},0],["QX",{"d":2}],["M",{"d":0},1],["QP",{"d":-2}],["M",{"d":0},2],["QC"],["M",{"d":0},3]]},"14":{"P":[["A",14,2],["B",14,0],["A",14,3],["B",14,1],["S3",10],["A",15,0],["B",14,2],["A",15,1],["B",14,3],["S3",11],["A",15,2],["B",15,0],["A",15,3],["S3",12],["B",15,1],["B",15,2],["B",15,3],["S3",13],["S3",14],["S3h",2],["S3h",3]],"S":[["C",14,2],["C",14,3],["O",10],["C",15,0],["C",15,1],["O",11],["C",15,2],["O",12],["C",15,3],["O",13],["O",14],["Oh",2]],"V":[["M",14,0],["QP",12],["M",14,1],["QP",13],["M",14,2],["M",14,3],["M",15,0],["M",15,1],["QP",14],["QPa",15],["M",15,2],["M",15,3],["QPc",15],["QPd",15],["Ohv",3]]},"15":{"P":[["NOP"]],"S":[["NOP"]],"V":[["NOP"]]}},"tail":{"P":[],"S":[],"V":[]},"vshare":[352,352,1],"pbf":4,"pq":6,"dma":[["w","a",0],["x","v",0,0,2],["w","b",0],["x","s",0,0,2],["x","v",0,2,4],["x","s",0,2,4],["x","v",1,0,2],["x","s",1,0,2],["w","a",1],["w","b",1],["x","v",1,2,4],["x","s",1,2,4],["c"]],"t3":3}
 NA = 3
 NB = 3
 NM = 2
@@ -131,7 +131,16 @@ def tile_vnclcell_pa_t_kernel(tc, v, s, Ca, Cb, Cc, out):
         def U(f, nl, which):
             c, g = divmod(f, 2)
             t, i = 2 * c + nl // 2, nl % 2
-            for w, o, nb in ((("a", 0, NA),) if which == "a" else (("b", 256, NB),)):
+            if which == "a":
+                bank["a", f, nl] = psum.tile([P, 512], F32, name="bka", tag="a", bufs=NA)
+                for jj in range(2):
+                    m = (4 * g + 2 * i + jj) * P
+                    nc.tensor.matmul_mx(out=bank["a", f, nl][:, jj * 256:(jj + 1) * 256],
+                                        lhsT=w_q["a"][:, m:m + P].bitcast(FP8X4), lhsT_scale=w_s["a"][:, m:m + P],
+                                        rhs=xq[t][:, 0:256].bitcast(FP8X4), rhs_scale=xs[t][:, 0:256],
+                                        start=True, stop=True)
+                return
+            for w, o, nb in (("b", 256, NB),):
                 bank[w, f, nl] = psum.tile([P, 512], F32, name="bk" + w, tag=w, bufs=nb)
                 for j in range(4):
                     m = (4 * g + j) * P
@@ -142,16 +151,17 @@ def tile_vnclcell_pa_t_kernel(tc, v, s, Ca, Cb, Cc, out):
                                         start=True, stop=True)
 
         def C(f, nl):
-            t3[f, nl] = ring.tile([P, 512], F32, name="t3", tag="t3", bufs=SPEC.get("t3", 3))
-            nc.scalar.copy(out=t3[f, nl][:].rearrange("p (w j) -> p w j", j=4),
-                           in_=bank["a", f, nl][:].rearrange("p (j w) -> p w j", j=4))
+            if nl % 2 == 0:
+                t3[f, nl // 2] = ring.tile([P, 4, 256], F32, name="t3", tag="t3", bufs=SPEC.get("t3", 3))
+            i = nl % 2
+            nc.scalar.copy(out=t3[f, nl // 2][:, 2 * i:2 * i + 2, :].rearrange("p j w -> p (j w)"), in_=bank["a", f, nl][:])
 
         def M(f, nl):
             if nl == 0:
                 pbf[f] = ring.tile([P, 2048], BF16, name="pbf", tag="pbf", bufs=SPEC.get("pbf", 3), align_bytes=64)
             nc.vector.tensor_tensor(out=pbf[f][:, 512 * nl:512 * nl + 512].rearrange("p (w j) -> p w j", j=4),
                                     in0=bank["b", f, nl][:].rearrange("p (j w) -> p w j", j=4),
-                                    in1=t3[f, nl][:].rearrange("p (w j) -> p w j", j=4), op=mybir.AluOpType.mult)
+                                    in1=t3[f, nl // 2][:, :, (nl % 2) * P:(nl % 2 + 1) * P].rearrange("p j w -> p w j"), op=mybir.AluOpType.mult)
 
         def QP(f, lo=0, hi=4):
             if lo == 0:
@@ -203,7 +213,7 @@ def tile_vnclcell_pa_t_kernel(tc, v, s, Ca, Cb, Cc, out):
                 add(("A", f, nl), "P", (lambda f=f, nl=nl: U(f, nl, "a")), [("QX", t), ("QW", "a", g)])
                 add(("B", f, nl), "P", (lambda f=f, nl=nl: U(f, nl, "b")), [("QX", t), ("QW", "b", g)])
                 add(("C", f, nl), "S", (lambda f=f, nl=nl: C(f, nl)), [("A", f, nl)])
-                add(("M", f, nl), "V", (lambda f=f, nl=nl: M(f, nl)), [("C", f, nl), ("B", f, nl)] + ([("M", f, nl - 1)] if nl else []))
+                add(("M", f, nl), "V", (lambda f=f, nl=nl: M(f, nl)), [("C", f, 2 * (nl // 2)), ("C", f, 2 * (nl // 2) + 1), ("B", f, nl)] + ([("M", f, nl - 1)] if nl else []))
             add(("QP", f), "V", (lambda f=f: QP(f)), [("M", f, 3)])
             add(("QPa", f), "V", (lambda f=f: QP(f, 0, 2)), [("M", f, 1)])
             add(("QPb", f), "V", (lambda f=f: QP(f, 2, 4)), [("M", f, 3), ("QPa", f)])
@@ -264,7 +274,9 @@ def tile_vnclcell_pa_t_kernel(tc, v, s, Ca, Cb, Cc, out):
             res = []
             if k in ("A", "B", "C"):
                 n = 4 * key[1] + key[2]
-                back = {"A": NA, "B": NB, "C": SPEC.get("t3", 3)}[k]
+                back = {"A": NA, "B": NB, "C": 2 * SPEC.get("t3", 3) - 1}[k]
+                if k == "C" and n % 2 == 1:
+                    back = n + 1
                 if n - back >= 0:
                     res.append(({"A": "C", "B": "M", "C": "M"}[k], (n - back) // 4, (n - back) % 4))
             if k in ("T", "S3", "S3h"):

@@ -152,16 +152,16 @@ def tile_vnclcell_pa_t_kernel(tc, v, s, Ca, Cb, Cc, out):
 
         def C(f, nl):
             if nl % 2 == 0:
-                t3[f, nl // 2] = ring.tile([P, 4, 256], F32, name="t3", tag="t3", bufs=SPEC.get("t3", 3))
-            i = nl % 2
-            nc.scalar.copy(out=t3[f, nl // 2][:, 2 * i:2 * i + 2, :].rearrange("p j w -> p (j w)"), in_=bank["a", f, nl][:])
+                t3[f, nl // 2] = ring.tile([P, 2, 256, 2], F32, name="t3", tag="t3", bufs=SPEC.get("t3", 3))
+            nc.scalar.copy(out=t3[f, nl // 2][:, nl % 2, :, :], in_=bank["a", f, nl][:].rearrange("p (e w) -> p w e", e=2))
 
         def M(f, nl):
             if nl == 0:
                 pbf[f] = ring.tile([P, 2048], BF16, name="pbf", tag="pbf", bufs=SPEC.get("pbf", 3), align_bytes=64)
-            nc.vector.tensor_tensor(out=pbf[f][:, 512 * nl:512 * nl + 512].rearrange("p (w j) -> p w j", j=4),
-                                    in0=bank["b", f, nl][:].rearrange("p (j w) -> p w j", j=4),
-                                    in1=t3[f, nl // 2][:, :, (nl % 2) * P:(nl % 2 + 1) * P].rearrange("p j w -> p w j"), op=mybir.AluOpType.mult)
+            nc.vector.tensor_tensor(out=pbf[f][:, 512 * nl:512 * nl + 512].rearrange("p (w h e) -> p w h e", h=2, e=2),
+                                    in0=bank["b", f, nl][:].rearrange("p (h e w) -> p w h e", h=2, e=2),
+                                    in1=t3[f, nl // 2][:, :, (nl % 2) * P:(nl % 2 + 1) * P, :].rearrange("p h w e -> p w h e"),
+                                    op=mybir.AluOpType.mult)
 
         def QP(f, lo=0, hi=4):
             if lo == 0:

@@ -10,326 +10,338 @@ U32 = mybir.dt.uint32
 FP8X4 = mybir.dt.float8_e4m3fn_x4
 
 P = 128
+PACK = 4
 B, K, R, H = 4096, 512, 1024, 256
-NSUB = B // P
+SUBTILES = B // P
+HALF = R // 2
+PHASES = SUBTILES // 2
+JOBS = SUBTILES // 2
+BANK = 512
 FLOPS = 2 * B * (2 * K * R + R * H)
-NPH = 16
-VSHARE = 352
-SPEC = {"banks":[3,3,2],"head":{"P":[["T",0],["T",1],["A",0,0],["A",0,1]],"S":[["RW","a",0],["Xv",0],["RW","b",0],["Xs",0],["Xv",1],["Xs",1],["C",0,0],["C",0,1]],"V":[["RW","a",0],["RW","b",0],["QW","a",0],["QX",0],["QW","b",0]]},"phase":{"P":[["T",{"d":2}],["A",{"d":0},2],["B",{"d":0},0],["A",{"d":0},3],["B",{"d":0},1],["S3",{"d":-4}],["A",{"d":1},0],["B",{"d":0},2],["A",{"d":1},1],["B",{"d":0},3]],"S":[["Xv",{"d":2}],["Xs",{"d":2}],["C",{"d":0},2],["C",{"d":0},3],["O",{"d":-4}],["C",{"d":1},0],["C",{"d":1},1]],"V":[["M",{"d":0},0],["QX",{"d":2}],["M",{"d":0},1],["M",{"d":0},2],["QP",{"d":-2}],["M",{"d":0},3]]},"phase_special":{"0":{"P":[["B",0,0],["B",0,1],["A",0,2],["A",0,3],["T",2],["B",0,2],["B",0,3],["A",1,0],["A",1,1]],"S":[["RW","a",1],["C",0,2],["C",0,3],["Xv",2],["Xs",2],["RW","b",1],["C",1,0],["C",1,1]],"V":[["QX",1],["RW","a",1],["M",0,0],["M",0,1],["QW","a",1],["RW","b",1],["M",0,2],["QX",2],["QW","b",1],["M",0,3]]},"1":{"V":[["M",{"d":0},0],["QX",{"d":2}],["M",{"d":0},1],["RC"],["M",{"d":0},2],["M",{"d":0},3]]},"3":{"V":[["M",{"d":0},0],["QX",{"d":2}],["M",{"d":0},1],["QP",{"d":-2}],["M",{"d":0},2],["QC"],["M",{"d":0},3]]},"14":{"P":[["A",14,2],["B",14,0],["A",14,3],["B",14,1],["S3",10],["A",15,0],["B",14,2],["A",15,1],["B",14,3],["S3",11],["A",15,2],["B",15,0],["A",15,3],["S3",12],["B",15,1],["B",15,2],["B",15,3],["S3",13],["S3",14],["S3h",2],["S3h",3]],"S":[["C",14,2],["C",14,3],["O",10],["C",15,0],["C",15,1],["O",11],["C",15,2],["O",12],["C",15,3],["O",13],["O",14],["Oh",2]],"V":[["M",14,0],["QP",12],["M",14,1],["QP",13],["M",14,2],["M",14,3],["M",15,0],["M",15,1],["QP",14],["QPa",15],["M",15,2],["M",15,3],["QPc",15],["QPd",15],["Ohv",3]]},"15":{"P":[["NOP"]],"S":[["NOP"]],"V":[["NOP"]]}},"tail":{"P":[],"S":[],"V":[]},"vshare":[352,352,1],"pbf":4,"pq":6,"dma":[["w","a",0],["x","v",0,0,2],["w","b",0],["x","s",0,0,2],["x","v",0,2,4],["x","s",0,2,4],["x","v",1,0,2],["x","s",1,0,2],["w","a",1],["w","b",1],["x","v",1,2,4],["x","s",1,2,4],["c"]],"t3":3}
-NA = 3
-NB = 3
-NM = 2
+
+T3_BANKS = 3
+T4_BANKS = 3
+OTHER_BANKS = 2
+
+VECTOR_COLUMNS = 352
 
 
 def tile_vnclcell_pa_t_kernel(tc, v, s, Ca, Cb, Cc, out):
     nc = tc.nc
     with ExitStack() as ctx:
         keep = ctx.enter_context(tc.tile_pool(name="keep", bufs=1))
-        ring = ctx.enter_context(tc.tile_pool(name="ring", bufs=2))
+        ring = ctx.enter_context(tc.tile_pool(name="ring", bufs=1))
         psum = ctx.enter_context(tc.psum_pool(name="psum", bufs=1))
         ctx.enter_context(tc.manual_schedule())
 
-        ident = keep.tile([P, P], F32, name="ident")
-        make_identity(nc, ident[:])
+        identity = keep.tile([P, P], F32, name="identity")
+        make_identity(nc, identity[:])
 
-        rows = {"v": v.rearrange("(p n) k -> p (n k)", n=NSUB), "s": s.rearrange("(p n) k -> p (n k)", n=NSUB)}
-        out_rows = out.rearrange("g (p n) h -> (g p) (n h)", n=NSUB)
-        wsrc = {"a": Ca, "b": Cb}
+        rows = {
+            "v": v.rearrange("(p n) k -> p (n k)", n=SUBTILES),
+            "s": s.rearrange("(p n) k -> p (n k)", n=SUBTILES),
+        }
+        out_rows = out.rearrange("g (p n) h -> (g p) (n h)", n=SUBTILES)
+        weights = {"a": Ca, "b": Cb}
 
         x_in = {}
-        for c in range(8):
+        for c in range(SUBTILES // 4):
             for x in "vs":
-                x_in[x, c] = keep.tile([P, 4 * K], BF16, name="x_%s%d" % (x, c))
+                x_in[x, c] = keep.tile([P, 4 * K], BF16, name="in_%s%d" % (x, c))
         w_raw = {}
-        w_q = {}
-        w_s = {}
+        w_codes = {}
+        w_scales = {}
         for w in "ab":
             for g in range(2):
-                w_raw[w, g] = keep.tile([P, 4, 512], BF16, name="raw_%s%d" % (w, g))
-            w_q[w] = keep.tile([P, R], U32, name="wq_" + w, align_bytes=64)
-            w_s[w] = keep.tile([P, R], U8, name="ws_" + w, align_bytes=64)
-        c_raw = keep.tile([P, 8, H], BF16, name="raw_c")
-        c_q = keep.tile([P, 2 * H], U32, name="cq", align_bytes=64)
-        c_s = keep.tile([P, 2 * H], U8, name="cs", align_bytes=64)
+                w_raw[w, g] = keep.tile([P, PACK, HALF], BF16, name="raw_%s%d" % (w, g))
+            w_codes[w] = keep.tile([P, R], U32, name="codes_" + w, align_bytes=64)
+            w_scales[w] = keep.tile([P, R], U8, name="scales_" + w, align_bytes=64)
+        c_raw = keep.tile([P, 2 * PACK, H], BF16, name="raw_c")
+        c_codes = keep.tile([P, 2 * H], U32, name="codes_c", align_bytes=64)
+        c_scales = keep.tile([P, 2 * H], U8, name="scales_c", align_bytes=64)
 
-        def load_x(x, c, lo, hi):
-            nc.sync.dma_start(out=x_in[x, c][:, lo * K:hi * K], in_=rows[x][:, (4 * c + lo) * K:(4 * c + hi) * K])
+        def load_rows(x, c, first, end):
+            nc.sync.dma_start(
+                out=x_in[x, c][:, first * K : end * K], in_=rows[x][:, (4 * c + first) * K : (4 * c + end) * K]
+            )
 
-        def load_w(w, g):
+        def load_weight(w, g):
             for u in range(2):
                 nc.sync.dma_start(
-                    out=w_raw[w, g][:, 2 * u:2 * u + 2, :],
-                    in_=wsrc[w][0, 256 * u:256 * u + 256, 512 * g:512 * g + 512].rearrange("(q e) c -> q e c", e=2))
+                    out=w_raw[w, g][:, 2 * u : 2 * u + 2, :],
+                    in_=weights[w][0, 256 * u : 256 * u + 256, HALF * g : HALF * (g + 1)].rearrange(
+                        "(q e) c -> q e c", e=2
+                    ),
+                )
 
-        for item in SPEC["dma"]:
-            if item[0] == "w":
-                load_w(item[1], item[2])
-            elif item[0] == "x":
-                load_x(item[1], item[2], item[3], item[4])
-            else:
-                nc.sync.dma_start(out=c_raw[:], in_=Cc[0, :, :].rearrange("(a p) h -> p a h", p=P))
-        for c in range(2, 8):
-            load_x("v", c, 0, 4)
-            load_x("s", c, 0, 4)
+        load_weight("a", 0)
+        load_rows("v", 0, 0, 2)
+        load_weight("b", 0)
+        load_rows("s", 0, 0, 2)
+        load_rows("v", 0, 2, 4)
+        load_rows("s", 0, 2, 4)
+        load_rows("v", 1, 0, 2)
+        load_rows("s", 1, 0, 2)
+        load_weight("a", 1)
+        load_weight("b", 1)
+        load_rows("v", 1, 2, 4)
+        load_rows("s", 1, 2, 4)
+        nc.sync.dma_start(out=c_raw[:], in_=Cc[0, :, :].rearrange("(a p) h -> p a h", p=P))
+        for c in range(2, SUBTILES // 4):
+            load_rows("v", c, 0, 4)
+            load_rows("s", c, 0, 4)
 
-        def regroup(copy, dst, src):
-            copy(out=dst.rearrange("p (c i t) -> p c t i", i=4, t=4), in_=src.rearrange("p t (c i) -> p c t i", i=4))
+        def regroup(copy, grouped, planes):
+            copy(
+                out=grouped.rearrange("p (c i t) -> p c t i", i=4, t=PACK),
+                in_=planes.rearrange("p t (c i) -> p c t i", i=4),
+            )
 
-        grp = {}
+        grouped_weights = {}
 
-        def w_regroup(w, g):
-            grp[w, g] = ring.tile([P, 2048], BF16, name="grp", tag="grp", bufs=3, align_bytes=64)
-            vs = SPEC["vshare"][g]
-            regroup(nc.vector.tensor_copy, grp[w, g][:, 0:4 * vs], w_raw[w, g][:, :, 0:vs])
-            regroup(nc.scalar.copy, grp[w, g][:, 4 * vs:2048], w_raw[w, g][:, :, vs:512])
+        def new_grouped_weights(key):
+            grouped_weights[key] = ring.tile([P, PACK * HALF], BF16, name="grouped_w", tag="grouped_w", bufs=3, align_bytes=64)
+            return grouped_weights[key]
 
-        def w_quant(w, g):
-            nc.vector.quantize_mx(out=w_q[w][:, 512 * g:512 * g + 512].bitcast(FP8X4), scales=w_s[w][:, 512 * g:512 * g + 512],
-                                  in_=grp[w, g][:])
+        def weight_regroup(w, g):
+            grouped = new_grouped_weights((w, g))
+            cut = VECTOR_COLUMNS
+            regroup(nc.vector.tensor_copy, grouped[:, 0 : PACK * cut], w_raw[w, g][:, :, 0:cut])
+            regroup(nc.scalar.copy, grouped[:, PACK * cut : PACK * HALF], w_raw[w, g][:, :, cut:HALF])
 
-        def c_regroup(copy):
-            grp["c"] = ring.tile([P, 2048], BF16, name="grp", tag="grp", bufs=3, align_bytes=64)
-            regroup(nc.vector.tensor_copy, grp["c"][:, 0:1024], c_raw[:, 0:4, :])
-            regroup(nc.vector.tensor_copy if SPEC["vshare"][2] else nc.scalar.copy, grp["c"][:, 1024:2048], c_raw[:, 4:8, :])
+        def weight_quantise(w, g):
+            cols = slice(HALF * g, HALF * (g + 1))
+            nc.vector.quantize_mx(
+                out=w_codes[w][:, cols].bitcast(FP8X4), scales=w_scales[w][:, cols], in_=grouped_weights[w, g][:]
+            )
 
-        def c_quant():
-            nc.vector.quantize_mx(out=c_q[:].bitcast(FP8X4), scales=c_s[:], in_=grp["c"][:])
+        def cc_regroup():
+            grouped = new_grouped_weights("c")
+            for g in range(2):
+                regroup(
+                    nc.vector.tensor_copy,
+                    grouped[:, PACK * H * g : PACK * H * (g + 1)],
+                    c_raw[:, PACK * g : PACK * (g + 1), :],
+                )
 
-        tb = {}
-        xg = {}
-        xq = {}
-        xs = {}
+        def cc_quantise():
+            nc.vector.quantize_mx(out=c_codes[:].bitcast(FP8X4), scales=c_scales[:], in_=grouped_weights["c"][:])
 
-        def T(t):
-            c, hp = divmod(t, 2)
+        words_t = {}
+        pair_grouped = {}
+        pair_codes = {}
+        pair_scales = {}
+
+        def transpose_pair(t):
+            c, second = divmod(t, 2)
             for x in "vs":
-                tb[x, t] = psum.tile([P, 512], F32, name="tb", tag="m", bufs=NM)
+                words_t[x, t] = psum.tile([P, BANK], F32, name="words_t", tag="other", bufs=OTHER_BANKS)
                 words = x_in[x, c][:].bitcast(F32)
                 for u in range(2):
                     for i in range(2):
-                        nc.tensor.transpose(tb[x, t][:, 256 * u + 128 * i:256 * u + 128 * i + 128],
-                                            words[:, (2 * hp + i) * 256 + 128 * u:(2 * hp + i) * 256 + 128 * u + 128], ident[:])
+                        first = (2 * second + i) * (K // 2) + P * u
+                        nc.tensor.transpose(
+                            words_t[x, t][:, 256 * u + P * i : 256 * u + P * (i + 1)],
+                            words[:, first : first + P],
+                            identity[:],
+                        )
 
-        def X(t, x, copy):
+        def copy_pair(t, x):
             if x == "v":
-                xg[t] = ring.tile([P, 2048], BF16, name="xg", tag="xg", bufs=3, align_bytes=64)
-            o = 0 if x == "v" else 512
-            copy(out=xg[t][:].bitcast(F32)[:, o:o + 512].rearrange("p (c u) -> p c u", u=2),
-                 in_=tb[x, t][:].rearrange("p (u c) -> p c u", u=2))
+                pair_grouped[t] = ring.tile([P, 2 * PACK * 256], BF16, name="pair_grouped", tag="pair_grouped", bufs=3, align_bytes=64)
+            first = 0 if x == "v" else BANK
+            nc.scalar.copy(
+                out=pair_grouped[t][:].bitcast(F32)[:, first : first + BANK].rearrange("p (c u) -> p c u", u=2),
+                in_=words_t[x, t][:].rearrange("p (u c) -> p c u", u=2),
+            )
 
-        def QX(t):
-            xq[t] = ring.tile([P, 512], U32, name="xq", tag="xq", bufs=6, align_bytes=64)
-            xs[t] = ring.tile([P, 512], U8, name="xs", tag="xs", bufs=6, align_bytes=64)
-            nc.vector.quantize_mx(out=xq[t][:].bitcast(FP8X4), scales=xs[t][:], in_=xg[t][:])
+        def quantise_pair(t):
+            pair_codes[t] = ring.tile([P, 2 * 256], U32, name="pair_codes", tag="pair_codes", bufs=6, align_bytes=64)
+            pair_scales[t] = ring.tile([P, 2 * 256], U8, name="pair_scales", tag="pair_scales", bufs=6, align_bytes=64)
+            nc.vector.quantize_mx(out=pair_codes[t][:].bitcast(FP8X4), scales=pair_scales[t][:], in_=pair_grouped[t][:])
 
-        bank = {}
-        t3 = {}
-        pbf = {}
-        pq = {}
-        ps = {}
+        def mx_pass(acc, w, tile_index, t, first, width):
+            m = slice(P * tile_index, P * (tile_index + 1))
+            n = slice(first, first + width)
+            nc.tensor.matmul_mx(
+                out=acc,
+                lhsT=w_codes[w][:, m].bitcast(FP8X4),
+                lhsT_scale=w_scales[w][:, m],
+                rhs=pair_codes[t][:, n].bitcast(FP8X4),
+                rhs_scale=pair_scales[t][:, n],
+                start=True,
+                stop=True,
+            )
 
-        def U(f, nl, which):
+        t3_bank = {}
+        t3_copy = {}
+        t4_bank = {}
+        product = {}
+        product_codes = {}
+        product_scales = {}
+
+        def t3_passes(f, pair, h):
             c, g = divmod(f, 2)
-            t, i = 2 * c + nl // 2, nl % 2
-            if which == "a":
-                bank["a", f, nl] = psum.tile([P, 512], F32, name="bka", tag="a", bufs=NA)
-                for jj in range(2):
-                    m = (4 * g + 2 * i + jj) * P
-                    nc.tensor.matmul_mx(out=bank["a", f, nl][:, jj * 256:(jj + 1) * 256],
-                                        lhsT=w_q["a"][:, m:m + P].bitcast(FP8X4), lhsT_scale=w_s["a"][:, m:m + P],
-                                        rhs=xq[t][:, 0:256].bitcast(FP8X4), rhs_scale=xs[t][:, 0:256],
-                                        start=True, stop=True)
-                return
-            for w, o, nb in (("b", 256, NB),):
-                bank[w, f, nl] = psum.tile([P, 512], F32, name="bk" + w, tag=w, bufs=nb)
-                for j in range(4):
-                    m = (4 * g + j) * P
-                    n = o + i * P
-                    nc.tensor.matmul_mx(out=bank[w, f, nl][:, j * P:(j + 1) * P],
-                                        lhsT=w_q[w][:, m:m + P].bitcast(FP8X4), lhsT_scale=w_s[w][:, m:m + P],
-                                        rhs=xq[t][:, n:n + P].bitcast(FP8X4), rhs_scale=xs[t][:, n:n + P],
-                                        start=True, stop=True)
+            t3_bank[f, pair, h] = psum.tile([P, BANK], F32, name="t3_bank", tag="t3", bufs=T3_BANKS)
+            for e in range(2):
+                mx_pass(t3_bank[f, pair, h][:, 256 * e : 256 * (e + 1)], "a", PACK * g + 2 * h + e, 2 * c + pair, 0, 256)
 
-        def C(f, nl):
-            if nl % 2 == 0:
-                t3[f, nl // 2] = ring.tile([P, 2, 256, 2], F32, name="t3", tag="t3", bufs=SPEC.get("t3", 3))
-            nc.scalar.copy(out=t3[f, nl // 2][:, nl % 2, :, :], in_=bank["a", f, nl][:].rearrange("p (e w) -> p w e", e=2))
+        def t3_copy_out(f, pair, h):
+            if h == 0:
+                t3_copy[f, pair] = ring.tile([P, 2, 256, 2], F32, name="t3_copy", tag="t3_copy", bufs=3)
+            nc.scalar.copy(
+                out=t3_copy[f, pair][:, h, :, :], in_=t3_bank[f, pair, h][:].rearrange("p (e w) -> p w e", e=2)
+            )
 
-        def M(f, nl):
-            if nl == 0:
-                pbf[f] = ring.tile([P, 2048], BF16, name="pbf", tag="pbf", bufs=SPEC.get("pbf", 3), align_bytes=64)
-            nc.vector.tensor_tensor(out=pbf[f][:, 512 * nl:512 * nl + 512].rearrange("p (w h e) -> p w h e", h=2, e=2),
-                                    in0=bank["b", f, nl][:].rearrange("p (h e w) -> p w h e", h=2, e=2),
-                                    in1=t3[f, nl // 2][:, :, (nl % 2) * P:(nl % 2 + 1) * P, :].rearrange("p h w e -> p w h e"),
-                                    op=mybir.AluOpType.mult)
+        def t4_passes(f, sub):
+            c, g = divmod(f, 2)
+            t4_bank[f, sub] = psum.tile([P, BANK], F32, name="t4_bank", tag="t4", bufs=T4_BANKS)
+            for j in range(PACK):
+                mx_pass(t4_bank[f, sub][:, P * j : P * (j + 1)], "b", PACK * g + j, 2 * c + sub // 2, 256 + P * (sub % 2), P)
 
-        def QP(f, lo=0, hi=4):
-            if lo == 0:
-                pq[f] = ring.tile([P, 512], U32, name="pq", tag="pq", bufs=SPEC.get("pq", 6), align_bytes=64)
-                ps[f] = ring.tile([P, 512], U8, name="ps", tag="ps", bufs=SPEC.get("pq", 6), align_bytes=64)
-            nc.vector.quantize_mx(out=pq[f][:, P * lo:P * hi].bitcast(FP8X4), scales=ps[f][:, P * lo:P * hi],
-                                  in_=pbf[f][:, 512 * lo:512 * hi])
+        def multiply(f, sub):
+            if sub == 0:
+                product[f] = ring.tile([P, 4 * BANK], BF16, name="product", tag="product", bufs=4, align_bytes=64)
+            i = sub % 2
+            nc.vector.tensor_tensor(
+                out=product[f][:, BANK * sub : BANK * (sub + 1)].rearrange("p (w h e) -> p w h e", h=2, e=2),
+                in0=t4_bank[f, sub][:].rearrange("p (h e w) -> p w h e", h=2, e=2),
+                in1=t3_copy[f, sub // 2][:, :, P * i : P * (i + 1), :].rearrange("p h w e -> p w h e"),
+                op=mybir.AluOpType.mult,
+            )
 
-        ob = {}
-        osb = {}
+        def quantise_product(f, first=0, end=4):
+            if first == 0:
+                product_codes[f] = ring.tile([P, 4 * P], U32, name="product_codes", tag="product_codes", bufs=6, align_bytes=64)
+                product_scales[f] = ring.tile([P, 4 * P], U8, name="product_scales", tag="product_scales", bufs=6, align_bytes=64)
+            nc.vector.quantize_mx(
+                out=product_codes[f][:, P * first : P * end].bitcast(FP8X4),
+                scales=product_scales[f][:, P * first : P * end],
+                in_=product[f][:, BANK * first : BANK * end],
+            )
 
-        def S3(c, lo, hi, tag="m", nb=NM):
-            ob[c, lo] = psum.tile([P, 512], F32, name="ob", tag=tag, bufs=nb)
-            for nl in range(lo, hi):
+        out_bank = {}
+
+        def third_matmul(n, count):
+            out_bank[n] = psum.tile([P, BANK], F32, name="out_bank", tag="other", bufs=OTHER_BANKS)
+            for i in range(count):
+                c, sub = divmod(n + i, 4)
                 for g in range(2):
-                    nc.tensor.matmul_mx(out=ob[c, lo][:, (nl - lo) * H:(nl - lo + 1) * H],
-                                        lhsT=pq[2 * c + g][:, nl * P:(nl + 1) * P].bitcast(FP8X4),
-                                        lhsT_scale=ps[2 * c + g][:, nl * P:(nl + 1) * P],
-                                        rhs=c_q[:, g * H:(g + 1) * H].bitcast(FP8X4), rhs_scale=c_s[:, g * H:(g + 1) * H],
-                                        start=(g == 0), stop=(g == 1))
+                    m = slice(P * sub, P * (sub + 1))
+                    nc.tensor.matmul_mx(
+                        out=out_bank[n][:, H * i : H * (i + 1)],
+                        lhsT=product_codes[2 * c + g][:, m].bitcast(FP8X4),
+                        lhsT_scale=product_scales[2 * c + g][:, m],
+                        rhs=c_codes[:, H * g : H * (g + 1)].bitcast(FP8X4),
+                        rhs_scale=c_scales[:, H * g : H * (g + 1)],
+                        start=(g == 0),
+                        stop=(g == 1),
+                    )
 
-        def O(c, lo, hi, copy):
-            w = (hi - lo) * H
-            osb[c, lo] = ring.tile([P, 512], F32, name="osb", tag="osb", bufs=4)
-            copy(out=osb[c, lo][:, 0:w], in_=ob[c, lo][:, 0:w])
-            nc.sync.dma_start(out=out_rows[:, (4 * c + lo) * H:(4 * c + hi) * H], in_=osb[c, lo][:, 0:w])
+        def store(n, count, copy):
+            out_tile = ring.tile([P, BANK], F32, name="out_tile", tag="out_tile", bufs=4)
+            copy(out=out_tile[:, 0 : H * count], in_=out_bank[n][:, 0 : H * count])
+            nc.sync.dma_start(out=out_rows[:, H * n : H * (n + count)], in_=out_tile[:, 0 : H * count])
 
-        vcopy = nc.vector.tensor_copy
-        scopy = nc.scalar.copy
+        def job(q):
+            third_matmul(2 * q, 2)
+            store(2 * q, 2, nc.scalar.copy)
 
-        ops = {}
-        def add(key, eng, fn, pre):
-            ops[key] = (eng, fn, pre)
-        for w in "ab":
-            for g in range(2):
-                add(("RW", w, g), "VS", (lambda w=w, g=g: w_regroup(w, g)), [])
-                add(("QW", w, g), "V", (lambda w=w, g=g: w_quant(w, g)), [("RW", w, g)])
-        add(("RC",), "V", (lambda: c_regroup(vcopy)), [])
-        add(("QC",), "V", c_quant, [("RC",)])
-        for t in range(16):
-            add(("T", t), "P", (lambda t=t: T(t)), [])
-            add(("Xv", t), "S", (lambda t=t: X(t, "v", scopy)), [("T", t)])
-            add(("Xs", t), "S", (lambda t=t: X(t, "s", scopy)), [("T", t), ("Xv", t)])
-            add(("QX", t), "V", (lambda t=t: QX(t)), [("Xs", t)])
-        for f in range(16):
-            c, g = divmod(f, 2)
-            for nl in range(4):
-                t = 2 * c + nl // 2
-                add(("A", f, nl), "P", (lambda f=f, nl=nl: U(f, nl, "a")), [("QX", t), ("QW", "a", g)])
-                add(("B", f, nl), "P", (lambda f=f, nl=nl: U(f, nl, "b")), [("QX", t), ("QW", "b", g)])
-                add(("C", f, nl), "S", (lambda f=f, nl=nl: C(f, nl)), [("A", f, nl)])
-                add(("M", f, nl), "V", (lambda f=f, nl=nl: M(f, nl)), [("C", f, 2 * (nl // 2)), ("C", f, 2 * (nl // 2) + 1), ("B", f, nl)] + ([("M", f, nl - 1)] if nl else []))
-            add(("QP", f), "V", (lambda f=f: QP(f)), [("M", f, 3)])
-            add(("QPa", f), "V", (lambda f=f: QP(f, 0, 2)), [("M", f, 1)])
-            add(("QPb", f), "V", (lambda f=f: QP(f, 2, 4)), [("M", f, 3), ("QPa", f)])
-            add(("QPc", f), "V", (lambda f=f: QP(f, 2, 3)), [("M", f, 2), ("QPa", f)])
-            add(("QPd", f), "V", (lambda f=f: QP(f, 3, 4)), [("M", f, 3), ("QPc", f)])
-        for q in range(16):
-            c = q // 2
-            add(("S3", q), "P", (lambda q=q: S3(q // 2, 2 * (q % 2), 2 * (q % 2) + 2)), [("QPx", 2 * c, q % 2), ("QPx", 2 * c + 1, q % 2), ("QC",)])
-            add(("O", q), "S", (lambda q=q: O(q // 2, 2 * (q % 2), 2 * (q % 2) + 2, scopy)), [("S3", q)])
-            add(("Ov", q), "V", (lambda q=q: O(q // 2, 2 * (q % 2), 2 * (q % 2) + 2, vcopy)), [("S3", q)])
-        for nl in (2, 3):
-            add(("S3h", nl), "P", (lambda nl=nl: S3(7, nl, nl + 1)), [("QPx", 14, 1), ("QPy", 15, nl), ("QC",)])
-            add(("Oh", nl), "S", (lambda nl=nl: O(7, nl, nl + 1, scopy)), [("S3h", nl)])
-            add(("Ohv", nl), "V", (lambda nl=nl: O(7, nl, nl + 1, vcopy)), [("S3h", nl)])
+        weight_regroup("a", 0)
+        transpose_pair(0)
+        copy_pair(0, "v")
+        weight_regroup("b", 0)
+        copy_pair(0, "s")
+        weight_quantise("a", 0)
+        quantise_pair(0)
+        weight_quantise("b", 0)
+        transpose_pair(1)
+        copy_pair(1, "v")
+        copy_pair(1, "s")
+        for h in range(2):
+            t3_passes(0, 0, h)
+        for h in range(2):
+            t3_copy_out(0, 0, h)
 
-        def expand(seq, f):
-            res = []
-            for item in seq:
-                nm, args = item[0], item[1:]
-                key = tuple([nm] + [(f + a["d"] if isinstance(a, dict) else a) for a in args])
-                res.append(key)
-            return res
+        quantise_pair(1)
+        weight_regroup("a", 1)
+        for sub in range(2):
+            t4_passes(0, sub)
+        for sub in range(2):
+            multiply(0, sub)
+        for h in range(2):
+            t3_passes(0, 1, h)
+        for h in range(2):
+            t3_copy_out(0, 1, h)
+        weight_quantise("a", 1)
+        transpose_pair(2)
+        copy_pair(2, "v")
+        copy_pair(2, "s")
+        weight_regroup("b", 1)
+        for sub in range(2, 4):
+            t4_passes(0, sub)
+        multiply(0, 2)
+        quantise_pair(2)
+        weight_quantise("b", 1)
+        multiply(0, 3)
+        for h in range(2):
+            t3_passes(1, 0, h)
+        for h in range(2):
+            t3_copy_out(1, 0, h)
 
-        queues = {"P": [], "S": [], "V": []}
-        for e in "PSV":
-            for key in SPEC["head"][e]:
-                queues[e].append(tuple(key))
-        for f in range(16):
-            for e in "PSV":
-                spec = SPEC["phase_special"].get(str(f), {}).get(e) or SPEC["phase"][e]
-                for key in expand(spec, f):
-                    if key[0] == "NOP": continue
-                    if key[0] in ("T", "Xv", "Xs", "QX") and not (0 <= key[1] < 16): continue
-                    if key[0] in ("S3", "O", "Ov") and not (0 <= key[1] < 16): continue
-                    if key[0] in ("QP", "A", "B", "C", "M") and not (0 <= key[1] < 16): continue
-                    queues[e].append(key)
-        for e in "PSV":
-            for key in SPEC["tail"][e]:
-                queues[e].append(tuple(key))
-        done = set()
+        for f in range(1, PHASES):
+            closing = f >= PHASES - 2
+            if not closing:
+                transpose_pair(f + 2)
+                copy_pair(f + 2, "v")
+                copy_pair(f + 2, "s")
 
-        def sat(p):
-            if p[0] == "QPx":
-                return ("QP", p[1]) in done or (("QPa", p[1]) in done if p[2] == 0 else (("QPb", p[1]) in done or ("QPd", p[1]) in done))
-            if p[0] == "QPy":
-                return ("QP", p[1]) in done or ("QPb", p[1]) in done or (("QPc", p[1]) in done if p[2] == 2 else ("QPd", p[1]) in done)
-            if p[0] == "Oany":
-                return ("O", p[1]) in done or ("Ov", p[1]) in done
-            if p[0] == "Ohany":
-                return ("Oh", p[1]) in done or ("Ohv", p[1]) in done
-            return p in done
+            t3_passes(f, 1, 0)
+            t3_copy_out(f, 1, 0)
+            t4_passes(f, 0)
+            multiply(f, 0)
+            if closing:
+                quantise_product(2 * f - PHASES)
+            else:
+                quantise_pair(f + 2)
+            t3_passes(f, 1, 1)
+            t3_copy_out(f, 1, 1)
+            t4_passes(f, 1)
+            multiply(f, 1)
+            if f == PHASES - 1:
+                quantise_product(f, 0, 2)
 
-        m_readers = []
-        grp_users = []
+            if closing:
+                job(2 * f - PHASES - 2)
+            elif f >= 4:
+                job(f - 4)
 
-        def reuse(key):
-            k = key[0]
-            res = []
-            if k in ("A", "B", "C"):
-                n = 4 * key[1] + key[2]
-                back = {"A": NA, "B": NB, "C": 2 * SPEC.get("t3", 3) - 1}[k]
-                if k == "C" and n % 2 == 1:
-                    back = n + 1
-                if n - back >= 0:
-                    res.append(({"A": "C", "B": "M", "C": "M"}[k], (n - back) // 4, (n - back) % 4))
-            if k in ("T", "S3", "S3h"):
-                need = 2 if k == "T" else 1
-                for i in range(need):
-                    j = len(m_readers) + i - NM
-                    if j >= 0:
-                        res.append(m_readers[j] if j < len(m_readers) else ("never",))
-            if k == "Xv" and key[1] >= 3:
-                res.append(("QX", key[1] - 3))
-            if k == "QX" and key[1] >= 6:
-                t = key[1] - 6
-                res.append(("B", 2 * (t // 2) + 1, 2 * (t % 2) + 1))
-            if k == "M" and key[2] == 0 and key[1] >= SPEC.get("pbf", 3):
-                res.append(("QPx", key[1] - SPEC.get("pbf", 3), 1))
-            if k in ("QP", "QPa") and key[1] >= SPEC.get("pq", 6):
-                res.append(("S3", 2 * ((key[1] - SPEC.get("pq", 6)) // 2) + 1))
-            if k in ("RW", "RC") and len(grp_users) >= 3:
-                res.append(grp_users[len(grp_users) - 3])
-            return res
+            if f + 1 < PHASES:
+                t3_passes(f + 1, 0, 0)
+                t3_copy_out(f + 1, 0, 0)
+            t4_passes(f, 2)
+            multiply(f, 2)
+            if f == 1:
+                cc_regroup()
+            elif f == PHASES - 2:
+                quantise_product(f - 1)
+            elif f < PHASES - 2:
+                quantise_product(f - 2)
+            if f == 3:
+                cc_quantise()
+            if f + 1 < PHASES:
+                t3_passes(f + 1, 0, 1)
+                t3_copy_out(f + 1, 0, 1)
+            t4_passes(f, 3)
+            multiply(f, 3)
 
-        def emitted(key):
-            k = key[0]
-            if k == "T":
-                m_readers.append(("Xv", key[1]))
-                m_readers.append(("Xs", key[1]))
-            if k == "S3":
-                m_readers.append(("Oany", key[1]))
-            if k == "S3h":
-                m_readers.append(("Ohany", key[1]))
-            if k == "RW":
-                grp_users.append(("QW", key[1], key[2]))
-            if k == "RC":
-                grp_users.append(("QC",))
-            done.add(key)
+            if closing:
+                job(2 * f - PHASES - 1)
 
-        pos = {"P": 0, "S": 0, "V": 0}
-        while any(pos[e] < len(queues[e]) for e in "PSV"):
-            prog = False
-            for e in "PSV":
-                if pos[e] >= len(queues[e]):
-                    continue
-                key = queues[e][pos[e]]
-                eng, fn, prq = ops[key]
-                if not all(sat(p) for p in list(prq) + reuse(key)):
-                    continue
-                if key[0] == "RW" or (key[0] == "RC" and not SPEC["vshare"][2]):
-                    other = "S" if e == "V" else "V"
-                    if not (pos[other] < len(queues[other]) and queues[other][pos[other]] == key):
-                        continue
-                    pos[other] += 1
-                fn()
-                emitted(key)
-                pos[e] += 1
-                prog = True
-            assert prog, "the three orders cannot be merged"
+        quantise_product(PHASES - 1, 2, 3)
+        quantise_product(PHASES - 1, 3, 4)
+        job(JOBS - 2)
+        third_matmul(SUBTILES - 2, 1)
+        third_matmul(SUBTILES - 1, 1)
+        store(SUBTILES - 2, 1, nc.scalar.copy)
+        store(SUBTILES - 1, 1, nc.vector.tensor_copy)

from contextlib import ExitStack

import concourse.mybir as mybir
from concourse.masks import make_identity

F32 = mybir.dt.float32
BF16 = mybir.dt.bfloat16
U8 = mybir.dt.uint8
U32 = mybir.dt.uint32
FP8X4 = mybir.dt.float8_e4m3fn_x4

P = 128
PACK = 4
B, K, R, H = 4096, 512, 1024, 256
SUBTILES = B // P
HALF = R // 2
PHASES = SUBTILES // 2
JOBS = SUBTILES // 2
BANK = 512
FLOPS = 2 * B * (2 * K * R + R * H)

T3_BANKS = 3
T4_BANKS = 3
OTHER_BANKS = 2

VECTOR_COLUMNS = 352


def tile_vnclcell_pa_t_kernel(tc, v, s, Ca, Cb, Cc, out):
    nc = tc.nc
    with ExitStack() as ctx:
        keep = ctx.enter_context(tc.tile_pool(name="keep", bufs=1))
        ring = ctx.enter_context(tc.tile_pool(name="ring", bufs=1))
        psum = ctx.enter_context(tc.psum_pool(name="psum", bufs=1))
        ctx.enter_context(tc.manual_schedule())

        identity = keep.tile([P, P], F32, name="identity")
        make_identity(nc, identity[:])

        rows = {
            "v": v.rearrange("(p n) k -> p (n k)", n=SUBTILES),
            "s": s.rearrange("(p n) k -> p (n k)", n=SUBTILES),
        }
        out_rows = out.rearrange("g (p n) h -> (g p) (n h)", n=SUBTILES)
        weights = {"a": Ca, "b": Cb}

        x_in = {}
        for c in range(SUBTILES // 4):
            for x in "vs":
                x_in[x, c] = keep.tile([P, 4 * K], BF16, name="in_%s%d" % (x, c))
        w_raw = {}
        w_codes = {}
        w_scales = {}
        for w in "ab":
            for g in range(2):
                w_raw[w, g] = keep.tile([P, PACK, HALF], BF16, name="raw_%s%d" % (w, g))
            w_codes[w] = keep.tile([P, R], U32, name="codes_" + w, align_bytes=64)
            w_scales[w] = keep.tile([P, R], U8, name="scales_" + w, align_bytes=64)
        c_raw = keep.tile([P, 2 * PACK, H], BF16, name="raw_c")
        c_codes = keep.tile([P, 2 * H], U32, name="codes_c", align_bytes=64)
        c_scales = keep.tile([P, 2 * H], U8, name="scales_c", align_bytes=64)

        def load_rows(x, c, first, end):
            nc.sync.dma_start(
                out=x_in[x, c][:, first * K : end * K], in_=rows[x][:, (4 * c + first) * K : (4 * c + end) * K]
            )

        def load_weight(w, g):
            for u in range(2):
                nc.sync.dma_start(
                    out=w_raw[w, g][:, 2 * u : 2 * u + 2, :],
                    in_=weights[w][0, 256 * u : 256 * u + 256, HALF * g : HALF * (g + 1)].rearrange(
                        "(q e) c -> q e c", e=2
                    ),
                )

        load_weight("a", 0)
        load_rows("v", 0, 0, 2)
        load_weight("b", 0)
        load_rows("s", 0, 0, 2)
        load_rows("v", 0, 2, 4)
        load_rows("s", 0, 2, 4)
        load_rows("v", 1, 0, 2)
        load_rows("s", 1, 0, 2)
        load_weight("a", 1)
        load_weight("b", 1)
        load_rows("v", 1, 2, 4)
        load_rows("s", 1, 2, 4)
        nc.sync.dma_start(out=c_raw[:], in_=Cc[0, :, :].rearrange("(a p) h -> p a h", p=P))
        for c in range(2, SUBTILES // 4):
            load_rows("v", c, 0, 4)
            load_rows("s", c, 0, 4)

        def regroup(copy, grouped, planes):
            copy(
                out=grouped.rearrange("p (c i t) -> p c t i", i=4, t=PACK),
                in_=planes.rearrange("p t (c i) -> p c t i", i=4),
            )

        grouped_weights = {}

        def new_grouped_weights(key):
            grouped_weights[key] = ring.tile([P, PACK * HALF], BF16, name="grouped_w", tag="grouped_w", bufs=3, align_bytes=64)
            return grouped_weights[key]

        def weight_regroup(w, g):
            grouped = new_grouped_weights((w, g))
            cut = VECTOR_COLUMNS
            regroup(nc.vector.tensor_copy, grouped[:, 0 : PACK * cut], w_raw[w, g][:, :, 0:cut])
            regroup(nc.scalar.copy, grouped[:, PACK * cut : PACK * HALF], w_raw[w, g][:, :, cut:HALF])

        def weight_quantise(w, g):
            cols = slice(HALF * g, HALF * (g + 1))
            nc.vector.quantize_mx(
                out=w_codes[w][:, cols].bitcast(FP8X4), scales=w_scales[w][:, cols], in_=grouped_weights[w, g][:]
            )

        def cc_regroup():
            grouped = new_grouped_weights("c")
            for g in range(2):
                regroup(
                    nc.vector.tensor_copy,
                    grouped[:, PACK * H * g : PACK * H * (g + 1)],
                    c_raw[:, PACK * g : PACK * (g + 1), :],
                )

        def cc_quantise():
            nc.vector.quantize_mx(out=c_codes[:].bitcast(FP8X4), scales=c_scales[:], in_=grouped_weights["c"][:])

        words_t = {}
        pair_grouped = {}
        pair_codes = {}
        pair_scales = {}

        def transpose_pair(t):
            c, second = divmod(t, 2)
            for x in "vs":
                words_t[x, t] = psum.tile([P, BANK], F32, name="words_t", tag="other", bufs=OTHER_BANKS)
                words = x_in[x, c][:].bitcast(F32)
                for u in range(2):
                    for i in range(2):
                        first = (2 * second + i) * (K // 2) + P * u
                        nc.tensor.transpose(
                            words_t[x, t][:, 256 * u + P * i : 256 * u + P * (i + 1)],
                            words[:, first : first + P],
                            identity[:],
                        )

        def copy_pair(t, x):
            if x == "v":
                pair_grouped[t] = ring.tile([P, 2 * PACK * 256], BF16, name="pair_grouped", tag="pair_grouped", bufs=3, align_bytes=64)
            first = 0 if x == "v" else BANK
            nc.scalar.copy(
                out=pair_grouped[t][:].bitcast(F32)[:, first : first + BANK].rearrange("p (c u) -> p c u", u=2),
                in_=words_t[x, t][:].rearrange("p (u c) -> p c u", u=2),
            )

        def quantise_pair(t):
            pair_codes[t] = ring.tile([P, 2 * 256], U32, name="pair_codes", tag="pair_codes", bufs=6, align_bytes=64)
            pair_scales[t] = ring.tile([P, 2 * 256], U8, name="pair_scales", tag="pair_scales", bufs=6, align_bytes=64)
            nc.vector.quantize_mx(out=pair_codes[t][:].bitcast(FP8X4), scales=pair_scales[t][:], in_=pair_grouped[t][:])

        def mx_pass(acc, w, tile_index, t, first, width):
            m = slice(P * tile_index, P * (tile_index + 1))
            n = slice(first, first + width)
            nc.tensor.matmul_mx(
                out=acc,
                lhsT=w_codes[w][:, m].bitcast(FP8X4),
                lhsT_scale=w_scales[w][:, m],
                rhs=pair_codes[t][:, n].bitcast(FP8X4),
                rhs_scale=pair_scales[t][:, n],
                start=True,
                stop=True,
            )

        t3_bank = {}
        t3_copy = {}
        t4_bank = {}
        product = {}
        product_codes = {}
        product_scales = {}

        def t3_passes(f, pair, h):
            c, g = divmod(f, 2)
            t3_bank[f, pair, h] = psum.tile([P, BANK], F32, name="t3_bank", tag="t3", bufs=T3_BANKS)
            for e in range(2):
                mx_pass(t3_bank[f, pair, h][:, 256 * e : 256 * (e + 1)], "a", PACK * g + 2 * h + e, 2 * c + pair, 0, 256)

        def t3_copy_out(f, pair, h):
            if h == 0:
                t3_copy[f, pair] = ring.tile([P, 2, 256, 2], F32, name="t3_copy", tag="t3_copy", bufs=3)
            nc.scalar.copy(
                out=t3_copy[f, pair][:, h, :, :], in_=t3_bank[f, pair, h][:].rearrange("p (e w) -> p w e", e=2)
            )

        def t4_passes(f, sub):
            c, g = divmod(f, 2)
            t4_bank[f, sub] = psum.tile([P, BANK], F32, name="t4_bank", tag="t4", bufs=T4_BANKS)
            for j in range(PACK):
                mx_pass(t4_bank[f, sub][:, P * j : P * (j + 1)], "b", PACK * g + j, 2 * c + sub // 2, 256 + P * (sub % 2), P)

        def multiply(f, sub):
            if sub == 0:
                product[f] = ring.tile([P, 4 * BANK], BF16, name="product", tag="product", bufs=4, align_bytes=64)
            i = sub % 2
            nc.vector.tensor_tensor(
                out=product[f][:, BANK * sub : BANK * (sub + 1)].rearrange("p (w h e) -> p w h e", h=2, e=2),
                in0=t4_bank[f, sub][:].rearrange("p (h e w) -> p w h e", h=2, e=2),
                in1=t3_copy[f, sub // 2][:, :, P * i : P * (i + 1), :].rearrange("p h w e -> p w h e"),
                op=mybir.AluOpType.mult,
            )

        def quantise_product(f, first=0, end=4):
            if first == 0:
                product_codes[f] = ring.tile([P, 4 * P], U32, name="product_codes", tag="product_codes", bufs=6, align_bytes=64)
                product_scales[f] = ring.tile([P, 4 * P], U8, name="product_scales", tag="product_scales", bufs=6, align_bytes=64)
            nc.vector.quantize_mx(
                out=product_codes[f][:, P * first : P * end].bitcast(FP8X4),
                scales=product_scales[f][:, P * first : P * end],
                in_=product[f][:, BANK * first : BANK * end],
            )

        out_bank = {}

        def third_matmul(n, count):
            out_bank[n] = psum.tile([P, BANK], F32, name="out_bank", tag="other", bufs=OTHER_BANKS)
            for i in range(count):
                c, sub = divmod(n + i, 4)
                for g in range(2):
                    m = slice(P * sub, P * (sub + 1))
                    nc.tensor.matmul_mx(
                        out=out_bank[n][:, H * i : H * (i + 1)],
                        lhsT=product_codes[2 * c + g][:, m].bitcast(FP8X4),
                        lhsT_scale=product_scales[2 * c + g][:, m],
                        rhs=c_codes[:, H * g : H * (g + 1)].bitcast(FP8X4),
                        rhs_scale=c_scales[:, H * g : H * (g + 1)],
                        start=(g == 0),
                        stop=(g == 1),
                    )

        def store(n, count, copy):
            out_tile = ring.tile([P, BANK], F32, name="out_tile", tag="out_tile", bufs=4)
            copy(out=out_tile[:, 0 : H * count], in_=out_bank[n][:, 0 : H * count])
            nc.sync.dma_start(out=out_rows[:, H * n : H * (n + count)], in_=out_tile[:, 0 : H * count])

        def job(q):
            third_matmul(2 * q, 2)
            store(2 * q, 2, nc.scalar.copy)

        weight_regroup("a", 0)
        transpose_pair(0)
        copy_pair(0, "v")
        weight_regroup("b", 0)
        copy_pair(0, "s")
        weight_quantise("a", 0)
        quantise_pair(0)
        weight_quantise("b", 0)
        transpose_pair(1)
        copy_pair(1, "v")
        copy_pair(1, "s")
        for h in range(2):
            t3_passes(0, 0, h)
        for h in range(2):
            t3_copy_out(0, 0, h)

        quantise_pair(1)
        weight_regroup("a", 1)
        for sub in range(2):
            t4_passes(0, sub)
        for sub in range(2):
            multiply(0, sub)
        for h in range(2):
            t3_passes(0, 1, h)
        for h in range(2):
            t3_copy_out(0, 1, h)
        weight_quantise("a", 1)
        transpose_pair(2)
        copy_pair(2, "v")
        copy_pair(2, "s")
        weight_regroup("b", 1)
        for sub in range(2, 4):
            t4_passes(0, sub)
        multiply(0, 2)
        quantise_pair(2)
        weight_quantise("b", 1)
        multiply(0, 3)
        for h in range(2):
            t3_passes(1, 0, h)
        for h in range(2):
            t3_copy_out(1, 0, h)

        for f in range(1, PHASES):
            closing = f >= PHASES - 2
            if not closing:
                transpose_pair(f + 2)
                copy_pair(f + 2, "v")
                copy_pair(f + 2, "s")

            t3_passes(f, 1, 0)
            t3_copy_out(f, 1, 0)
            t4_passes(f, 0)
            multiply(f, 0)
            if closing:
                quantise_product(2 * f - PHASES)
            else:
                quantise_pair(f + 2)
            t3_passes(f, 1, 1)
            t3_copy_out(f, 1, 1)
            t4_passes(f, 1)
            multiply(f, 1)
            if f == PHASES - 1:
                quantise_product(f, 0, 2)

            if closing:
                job(2 * f - PHASES - 2)
            elif f >= 4:
                job(f - 4)

            if f + 1 < PHASES:
                t3_passes(f + 1, 0, 0)
                t3_copy_out(f + 1, 0, 0)
            t4_passes(f, 2)
            multiply(f, 2)
            if f == 1:
                cc_regroup()
            elif f == PHASES - 2:
                quantise_product(f - 1)
            elif f < PHASES - 2:
                quantise_product(f - 2)
            if f == 3:
                cc_quantise()
            if f + 1 < PHASES:
                t3_passes(f + 1, 0, 1)
                t3_copy_out(f + 1, 0, 1)
            t4_passes(f, 3)
            multiply(f, 3)

            if closing:
                job(2 * f - PHASES - 1)

        quantise_product(PHASES - 1, 2, 3)
        quantise_product(PHASES - 1, 3, 4)
        job(JOBS - 2)
        third_matmul(SUBTILES - 2, 1)
        third_matmul(SUBTILES - 1, 1)
        store(SUBTILES - 2, 1, nc.scalar.copy)
        store(SUBTILES - 1, 1, nc.vector.tensor_copy)
